import numpy as np
import ml_dtypes


def mxq(x, axis, fmt="e4m3"):
    dtype, down = {"e4m3": (ml_dtypes.float8_e4m3fn, 7), "e5m2": (ml_dtypes.float8_e5m2, 14)}[fmt]
    v = np.moveaxis(np.asarray(x, np.float32).astype(ml_dtypes.bfloat16).astype(np.float64), axis, -1)
    blocks = v.reshape(v.shape[:-1] + (-1, 32))
    amax = np.abs(blocks).max(-1, keepdims=True)
    byte = np.maximum(np.where(amax > 0, np.frexp(amax)[1] - 1 + 127, 0) - down, 1)
    scale = np.exp2(byte - 127.0)
    codes = (blocks / scale).astype(np.float32).astype(dtype).astype(np.float64)
    return np.moveaxis((codes * scale).reshape(v.shape), -1, axis)


WIDE = False


def mx_kscale(k):
    if not WIDE:
        return np.ones(k)
    levels = np.array([10, -10, 5, -5, 0])
    if k % 512:
        return np.exp2(np.random.permutation(np.resize(levels, k // 32))).repeat(32)
    a = np.empty((k // 512, 16))
    for p in range(k // 512):
        a[p, :8] = np.random.permutation(np.resize(levels, 8))
        for g in range(8):
            far = levels[np.abs(levels - a[p, g]) >= 10]
            a[p, g + 8] = far[np.random.randint(len(far))]
    return np.exp2(a.ravel()).repeat(32)


BF16 = ml_dtypes.bfloat16


def bf(x):
    return np.asarray(x, np.float32).astype(BF16)


def f64(x):
    return np.asarray(x).astype(np.float64)


B, IN, HID, PROJ, H, KC = 4096, 2048, 128, 512, 1, 4
BH = HID // H
BI = PROJ // H


def sigmoid(v):
    return 1.0 / (1.0 + np.exp(-v))


def silu(v):
    return v / (1.0 + np.exp(-v))


def blockdiag(vq, w, b):
    y = vq.reshape(B, H, BI).transpose(1, 0, 2) @ mxq(f64(w), 1, "e4m3")
    return y.transpose(1, 0, 2).reshape(B, HID) + f64(b)


def setup_inputs():
    s, t = mx_kscale(PROJ), mx_kscale(PROJ)
    sh, th = s.reshape(H, BI, 1), t.reshape(H, BI, 1)
    r = np.random.standard_normal
    return {"x_conv": bf(silu(r((B, PROJ))) * s), "x_left": bf(r((B, PROJ)) * t),
            "c_prev": bf(r((B, HID))), "n_prev": bf(r((B, HID))), "m_prev": bf(0.5 * r((B, HID))),
            "wq_w": bf(r((H, BI, BH)) * 1.5 / np.sqrt(BI) / sh), "wq_b": bf(0.2 * r(HID)),
            "wk_w": bf(r((H, BI, BH)) * 0.5 * np.sqrt(BH) / np.sqrt(BI) / sh), "wk_b": bf(0.1 * np.sqrt(BH) * r(HID)),
            "wv_w": bf(r((H, BI, BH)) / np.sqrt(BI) / th), "wv_b": bf(0.2 * r(HID)),
            "wi_w": bf(r((PROJ, HID)) * 1.5 / np.sqrt(PROJ) / s[:, None]), "wi_b": bf(0.2 * r(HID)),
            "wf_w": bf(r((PROJ, HID)) * 1.5 / np.sqrt(PROJ) / s[:, None]), "wf_b": bf(0.2 * r(HID)),
            "wo_w": bf(r((PROJ, HID)) / np.sqrt(PROJ) / t[:, None]), "wo_b": bf(0.2 * r(HID))}


def reference(x_conv, x_left, c_prev, n_prev, m_prev, wq_w, wq_b, wk_w, wk_b, wv_w, wv_b, wi_w, wi_b, wf_w, wf_b, wo_w, wo_b):
    xc = mxq(f64(x_conv), 1, "e4m3")
    xl = mxq(f64(x_left), 1, "e4m3")
    q = blockdiag(xc, wq_w, wq_b)
    k = blockdiag(xc, wk_w, wk_b) / np.sqrt(BH)
    v = blockdiag(xl, wv_w, wv_b)
    i_tilde = (xc @ mxq(f64(wi_w), 0, "e4m3")) + f64(wi_b)
    f_tilde = (xc @ mxq(f64(wf_w), 0, "e4m3")) + f64(wf_b)
    o = sigmoid((xl @ mxq(f64(wo_w), 0, "e4m3")) + f64(wo_b))
    m_t = np.maximum(f_tilde + f64(m_prev), i_tilde)
    i = np.exp(i_tilde - m_t)
    f = np.exp(f_tilde + f64(m_prev) - m_t)
    c_t = f * f64(c_prev) + i * (v * k)
    n_t = f * f64(n_prev) + i * k
    denom = np.sqrt(np.sum((n_t * q) ** 2, axis=-1, keepdims=True)) + 1e-6
    h_t = o * (c_t * q) / denom
    return h_t, c_t, n_t, m_t

@@ -1,0 +1,436 @@
+import math
+
+import concourse.mybir as mybir
+from concourse.masks import make_identity
+
+FP8X4 = mybir.dt.float8_e4m3fn_x4
+BF16 = mybir.dt.bfloat16
+F32 = mybir.dt.float32
+U32 = mybir.dt.uint32
+U8 = mybir.dt.uint8
+ALU = mybir.AluOpType
+ACT = mybir.ActivationFunctionType
+
+P = 128
+ROWS = 4096
+K = 512
+H = 128
+TILES = ROWS // P
+TPC = 4
+CHUNKS = TILES // TPC
+CW = TPC * H
+GATES = 6
+G_I, G_F, G_K, G_Q, G_V, G_O = 0, 1, 2, 3, 4, 5
+FLOPS = 2 * ROWS * K * H * GATES
+
+
+def tile_mlstmblock_pb_t_kernel(
+    tc,
+    x_conv,
+    x_left,
+    c_prev,
+    n_prev,
+    m_prev,
+    wq_w,
+    wq_b,
+    wk_w,
+    wk_b,
+    wv_w,
+    wv_b,
+    wi_w,
+    wi_b,
+    wf_w,
+    wf_b,
+    wo_w,
+    wo_b,
+    out_0,
+    out_1,
+    out_2,
+    out_3,
+):
+    nc = tc.nc
+    k_scale = 1.0 / math.sqrt(float(H))
+
+    def by_partition(dram):
+        return dram.rearrange("(p t) w -> p t w", t=TILES)
+
+    x_views = {"c": by_partition(x_conv), "l": by_partition(x_left)}
+    state_views = {"m": by_partition(m_prev), "n": by_partition(n_prev), "c": by_partition(c_prev)}
+    out_views = {
+        "h": by_partition(out_0),
+        "c": by_partition(out_1),
+        "n": by_partition(out_2),
+        "m": by_partition(out_3),
+    }
+    weights = [None] * GATES
+    biases = [None] * GATES
+    for g, w_ap, b_ap in (
+        (G_I, wi_w, wi_b),
+        (G_F, wf_w, wf_b),
+        (G_K, wk_w[0], wk_b),
+        (G_Q, wq_w[0], wq_b),
+        (G_V, wv_w[0], wv_b),
+        (G_O, wo_w, wo_b),
+    ):
+        weights[g] = w_ap
+        biases[g] = b_ap
+
+    with tc.tile_pool(name="const", bufs=1) as const, tc.tile_pool(
+        name="xin", bufs=3
+    ) as xin, tc.tile_pool(name="state", bufs=CHUNKS // 2) as state, tc.tile_pool(
+        name="quant", bufs=2
+    ) as quant, tc.tile_pool(name="work", bufs=2) as work, tc.tile_pool(
+        name="outs", bufs=3
+    ) as outs, tc.psum_pool(name="front", bufs=3) as front, tc.psum_pool(
+        name="gate", bufs=1
+    ) as gate, tc.psum_pool(name="rows", bufs=3) as rows, tc.manual_schedule():
+        kept = {}
+
+        def absent(c):
+            return c < 0 or c >= CHUNKS
+
+        def by_tile(ap):
+            return ap.rearrange("p (t h) -> p t h", h=H)
+
+        def new(pool, name, c):
+            kept[(name, c)] = pool.tile([P, CW], F32, tag=name, name=name)
+            return kept[(name, c)]
+
+        def load_x(c, nm):
+            if absent(c):
+                return
+            x_sb = xin.tile([P, TPC * K], BF16, tag="x" + nm, name="x" + nm)
+            nc.sync.dma_start(
+                out=x_sb[:].rearrange("p (t k) -> p t k", t=TPC),
+                in_=x_views[nm][:, c * TPC : (c + 1) * TPC, :],
+            )
+            kept[("x" + nm, c)] = x_sb
+
+        def load_state(c):
+            if absent(c) or c % 2 == 1:
+                return
+            for nm in ("n", "c"):
+                st = state.tile([P, 2 * CW], BF16, tag="st" + nm, name="st" + nm)
+                nc.sync.dma_start(out=by_tile(st[:]), in_=state_views[nm][:, c * TPC : (c + 2) * TPC, :])
+                kept[(nm + "_prev", c)] = st[:, 0:CW]
+                kept[(nm + "_prev", c + 1)] = st[:, CW : 2 * CW]
+
+        m_all = const.tile([P, CHUNKS * CW], BF16)
+
+        def load_m(first, count):
+            nc.sync.dma_start(
+                out=by_tile(m_all[:, first * CW : (first + count) * CW]),
+                in_=state_views["m"][:, first * TPC : (first + count) * TPC, :],
+            )
+
+        def store(c, nm):
+            if absent(c):
+                return
+            nc.sync.dma_start(
+                out=out_views[nm][:, c * TPC : (c + 1) * TPC, :], in_=by_tile(kept[(nm + "_t", c)][:])
+            )
+
+        load_x(0, "c")
+        bias_rows = const.tile([P, P], BF16)
+        nc.vector.memset(bias_rows[:], 0.0)
+        for g in range(GATES):
+            nc.sync.dma_start(out=bias_rows[g : g + 1, :], in_=biases[g].unsqueeze(0))
+        w_raw = const.tile([P, GATES, 4, H], BF16)
+        for g in range(GATES):
+            nc.sync.dma_start(
+                out=w_raw[:, g, :, :],
+                in_=weights[g].rearrange("(q j) c -> q j c", j=4),
+            )
+        load_x(0, "l")
+        load_m(0, CHUNKS // 2)
+        load_state(0)
+        load_x(1, "c")
+        load_x(1, "l")
+        load_m(CHUNKS // 2, CHUNKS // 2)
+        load_x(2, "c")
+        load_x(2, "l")
+
+        zero = const.tile([P, 1], F32)
+        nc.vector.memset(zero[:], 0.0)
+        one = const.tile([P, 1], F32)
+        nc.scalar.activation(out=one[:], in_=zero[:], func=ACT.Exp)
+        half = const.tile([P, TPC], F32)
+        nc.vector.memset(half[:], 0.5)
+        ident = const.tile([P, P], F32)
+        make_identity(nc, ident[:])
+        ident_bf = const.tile([P, P], BF16)
+        nc.vector.tensor_copy(out=ident_bf[:], in_=ident[:])
+
+        bias_f32 = const.tile([P, P], F32)
+        nc.vector.tensor_copy(out=bias_f32[:], in_=bias_rows[:])
+        spread = rows.tile([P, CW], F32, tag="rows", name="spread")
+        nc.tensor.transpose(spread[:, 0:P], bias_f32[:], ident[:])
+        for g in (G_I, G_F):
+            nc.tensor.matmul(
+                out=spread[:, (g + 1) * P : (g + 2) * P],
+                lhsT=ident_bf[:, g : g + 1].to_broadcast([P, P]),
+                rhs=bias_rows[:],
+                start=True,
+                stop=True,
+            )
+
+        w_grouped = const.tile([P, GATES, H, 4], BF16, align_bytes=64)
+        w_codes = const.tile([P, GATES * H], U32, align_bytes=64)
+        w_scales = const.tile([P, GATES * H], U8, align_bytes=64)
+
+        def quantise_weights(g0, g1):
+            nc.vector.tensor_copy(
+                out=w_grouped[:, g0:g1], in_=w_raw[:, g0:g1].rearrange("p g t c -> p g c t")
+            )
+            nc.vector.quantize_mx(
+                out=w_codes[:, g0 * H : g1 * H].bitcast(FP8X4),
+                scales=w_scales[:, g0 * H : g1 * H],
+                in_=w_grouped[:, g0:g1].rearrange("p g c t -> p (g c t)"),
+            )
+
+        quantise_weights(G_I, G_F + 1)
+        bias_col = const.tile([P, GATES], F32)
+        nc.vector.tensor_copy(out=bias_col[:], in_=spread[:, 0:GATES])
+        bk_scaled = const.tile([P, 1], F32)
+        nc.vector.tensor_scalar_mul(out=bk_scaled[:], in0=bias_col[:, G_K : G_K + 1], scalar1=k_scale)
+        bo_half = const.tile([P, 1], F32)
+        nc.vector.tensor_scalar_mul(out=bo_half[:], in0=bias_col[:, G_O : G_O + 1], scalar1=0.5)
+        bi_row = const.tile([P, H], F32)
+        nc.vector.tensor_copy(out=bi_row[:], in_=spread[:, (G_I + 1) * P : (G_I + 2) * P])
+        bf_minus_bi_row = const.tile([P, H], F32)
+        nc.vector.tensor_tensor(
+            out=bf_minus_bi_row[:], in0=spread[:, (G_F + 1) * P : (G_F + 2) * P], in1=bi_row[:], op=ALU.subtract
+        )
+        quantise_weights(G_K, G_Q + 1)
+        quantise_weights(G_V, G_O + 1)
+
+        def over_tiles(row):
+            return row[:].unsqueeze(1).to_broadcast([P, TPC, H])
+
+        m_shifted = const.tile([P, CHUNKS * CW], F32)
+        for c in range(CHUNKS):
+            nc.gpsimd.tensor_tensor(
+                out=by_tile(m_shifted[:, c * CW : (c + 1) * CW]),
+                in0=by_tile(m_all[:, c * CW : (c + 1) * CW]),
+                in1=over_tiles(bf_minus_bi_row),
+                op=ALU.add,
+            )
+            kept[("m_shifted", c)] = m_shifted[:, c * CW : (c + 1) * CW]
+
+        def transpose_x(c, nm, half_no):
+            if absent(c):
+                return
+            words = kept[("x" + nm, c)][:].bitcast(F32)
+            bank = front.tile([P, CW], F32, tag="front", name="xT")
+            for tt in range(2):
+                t = 2 * half_no + tt
+                for u in range(2):
+                    nc.tensor.transpose(
+                        bank[:, u * 256 + tt * P : u * 256 + (tt + 1) * P],
+                        words[:, t * 256 + u : (t + 1) * 256 : 2],
+                        ident[:],
+                    )
+            kept[("xT" + nm, c, half_no)] = bank
+
+        def regroup_x(c, nm, half_no):
+            if absent(c):
+                return
+            if half_no == 0:
+                kept[("grouped" + nm, c)] = quant.tile(
+                    [P, 4 * CW], BF16, tag="grouped" + nm, name="grouped" + nm, align_bytes=64
+                )
+            words = kept[("grouped" + nm, c)][:].bitcast(F32)
+            nc.scalar.copy(
+                out=words[:, half_no * CW : (half_no + 1) * CW].rearrange("p (b u) -> p b u", u=2),
+                in_=kept[("xT" + nm, c, half_no)][:].rearrange("p (u b) -> p b u", u=2),
+            )
+
+        def quantise_x(c, nm):
+            if absent(c):
+                return
+            codes = quant.tile([P, CW], U32, tag="codes" + nm, name="codes" + nm, align_bytes=64)
+            scales = quant.tile([P, CW], U8, tag="scales" + nm, name="scales" + nm, align_bytes=64)
+            nc.vector.quantize_mx(
+                out=codes[:].bitcast(FP8X4), scales=scales[:], in_=kept[("grouped" + nm, c)][:]
+            )
+            kept[("mx" + nm, c)] = (codes, scales)
+
+        def project_rows(c, g, nm, name):
+            if absent(c):
+                return
+            codes, scales = kept[("mx" + nm, c)]
+            acc = gate.tile([P, CW], F32, tag=name, name=name)
+            for t in range(TPC):
+                nc.tensor.matmul_mx(
+                    out=acc[:, t * H : (t + 1) * H],
+                    lhsT=codes[:, t * P : (t + 1) * P].bitcast(FP8X4),
+                    lhsT_scale=scales[:, t * P : (t + 1) * P],
+                    rhs=w_codes[:, g * H : (g + 1) * H].bitcast(FP8X4),
+                    rhs_scale=w_scales[:, g * H : (g + 1) * H],
+                    start=True,
+                    stop=True,
+                )
+            kept[(name, c)] = acc
+
+        def project_cols(c, g, nm, name, func, bias_ap, scale):
+            if absent(c):
+                return
+            codes, scales = kept[("mx" + nm, c)]
+            acc = front.tile([P, CW], F32, tag="front", name="acc")
+            nc.tensor.matmul_mx(
+                out=acc[:],
+                lhsT=w_codes[:, g * H : (g + 1) * H].bitcast(FP8X4),
+                lhsT_scale=w_scales[:, g * H : (g + 1) * H],
+                rhs=codes[:].bitcast(FP8X4),
+                rhs_scale=scales[:],
+                start=True,
+                stop=True,
+            )
+            kept[("acc" + name, c)] = (acc, func, bias_ap, scale)
+
+        def leave_psum(c, name):
+            if absent(c):
+                return
+            acc, func, bias_ap, scale = kept[("acc" + name, c)]
+            nc.scalar.activation(
+                out=new(work, name + "_cols", c)[:], in_=acc[:], func=func, bias=bias_ap, scale=scale
+            )
+
+        def to_rows(c, name):
+            if absent(c):
+                return
+            src = kept[(name + "_cols", c)]
+            bank = rows.tile([P, CW], F32, tag="rows", name=name + "_rows")
+            for t in range(TPC):
+                nc.tensor.transpose(bank[:, t * H : (t + 1) * H], src[:, t * P : (t + 1) * P], ident[:])
+            kept[(name, c)] = bank
+
+        def tensor_tensor(engine, pool, out_name, c, a, b, op):
+            if absent(c):
+                return
+            engine.tensor_tensor(out=new(pool, out_name, c)[:], in0=kept[(a, c)][:], in1=kept[(b, c)][:], op=op)
+
+        def scalar_then_tensor(pool, out_name, c, a, scalar, op0, b, op1):
+            if absent(c):
+                return
+            nc.vector.scalar_tensor_tensor(
+                out=new(pool, out_name, c)[:],
+                in0=kept[(a, c)][:],
+                scalar=scalar,
+                in1=kept[(b, c)][:],
+                op0=op0,
+                op1=op1,
+            )
+
+        def add_row(pool, out_name, c, a, row):
+            if absent(c):
+                return
+            nc.gpsimd.tensor_tensor(
+                out=by_tile(new(pool, out_name, c)[:]), in0=by_tile(kept[(a, c)][:]), in1=over_tiles(row), op=ALU.add
+            )
+
+        def exponential(c, out_name, sign):
+            if absent(c):
+                return
+            nc.scalar.activation(out=new(work, out_name, c)[:], in_=kept[("d", c)][:], func=ACT.Exp, scale=sign)
+
+        def sum_of_squares(c):
+            if absent(c):
+                return
+            squares = work.tile([P, CW], F32, tag="squares", name="squares")
+            ss = work.tile([P, TPC], F32, tag="ss", name="ss")
+            for t in range(TPC):
+                nc.scalar.activation(
+                    out=squares[:, t * H : (t + 1) * H],
+                    in_=kept[("nq", c)][:, t * H : (t + 1) * H],
+                    func=ACT.Square,
+                    scale=2.0,
+                    accum_out=ss[:, t : t + 1],
+                )
+            kept[("ss", c)] = ss
+
+        def small(c, name):
+            kept[(name, c)] = work.tile([P, TPC], F32, tag=name, name=name)
+            return kept[(name, c)]
+
+        def square_root(c):
+            if absent(c):
+                return
+            nc.gpsimd.tensor_tensor(out=small(c, "root")[:], in0=kept[("ss", c)][:], in1=half[:], op=ALU.pow)
+
+        def add_epsilon(c):
+            if absent(c):
+                return
+            nc.vector.tensor_scalar_add(out=small(c, "denom2")[:], in0=kept[("root", c)][:], scalar1=2.0e-6)
+
+        def reciprocal(c):
+            if absent(c):
+                return
+            nc.vector.reciprocal(out=small(c, "scale")[:], in_=kept[("denom2", c)][:])
+
+        def scale_rows(c):
+            if absent(c):
+                return
+            h_t = new(outs, "h_t", c)
+            for t in range(TPC):
+                nc.vector.tensor_scalar_mul(
+                    out=h_t[:, t * H : (t + 1) * H],
+                    in0=kept[("h_unscaled", c)][:, t * H : (t + 1) * H],
+                    scalar1=kept[("scale", c)][:, t : t + 1],
+                )
+
+        for j in range(-2, CHUNKS + 2):
+            ahead, gates, cell, last, done = j + 2, j + 1, j, j - 1, j - 2
+
+            tensor_tensor(nc.vector, work, "u", gates, "f_sum", "m_shifted", ALU.add)
+            scalar_then_tensor(work, "ik", cell, "exp_minus_d", 1.0, ALU.min, "k", ALU.mult)
+            tensor_tensor(nc.vector, work, "d", gates, "u", "i_sum", ALU.subtract)
+            scalar_then_tensor(work, "fn", cell, "exp_d", 1.0, ALU.min, "n_prev", ALU.mult)
+            tensor_tensor(nc.vector, work, "nq", last, "q", "n_t", ALU.mult)
+            leave_psum(gates, "k")
+            to_rows(cell, "v")
+            tensor_tensor(nc.gpsimd, outs, "n_t", cell, "fn", "ik", ALU.add)
+
+            for nm in ("c", "l"):
+                for half_no in range(2):
+                    transpose_x(ahead, nm, half_no)
+                    regroup_x(ahead, nm, half_no)
+            load_x(j + 5, "c")
+            load_x(j + 5, "l")
+            load_state(j + 4)
+            store(cell, "n")
+
+            tensor_tensor(nc.vector, work, "ikv", cell, "v", "ik", ALU.mult)
+            scalar_then_tensor(work, "m_less_bi", gates, "d", 0.0, ALU.max, "i_sum", ALU.add)
+            scalar_then_tensor(work, "fc", cell, "exp_d", 1.0, ALU.min, "c_prev", ALU.mult)
+            tensor_tensor(nc.vector, work, "cq", last, "q", "c_t", ALU.mult)
+            add_row(outs, "m_t", gates, "m_less_bi", bi_row)
+            tensor_tensor(nc.gpsimd, outs, "c_t", cell, "fc", "ikv", ALU.add)
+
+            to_rows(last, "o")
+            project_cols(gates, G_V, "l", "v", ACT.Identity, bias_col[:, G_V : G_V + 1], 1.0)
+            leave_psum(gates, "v")
+            project_cols(gates, G_O, "l", "o", ACT.Tanh, bo_half[:], 0.5)
+            leave_psum(gates, "o")
+            project_cols(gates, G_Q, "c", "q", ACT.Identity, bias_col[:, G_Q : G_Q + 1], 1.0)
+            leave_psum(gates, "q")
+            to_rows(gates, "k")
+
+            quantise_x(ahead, "c")
+            add_epsilon(done)
+            scalar_then_tensor(work, "h_unscaled", last, "o", 1.0, ALU.add, "cq", ALU.mult)
+            reciprocal(done)
+            quantise_x(ahead, "l")
+            scale_rows(done)
+            sum_of_squares(last)
+            exponential(gates, "exp_minus_d", -1.0)
+            exponential(gates, "exp_d", 1.0)
+            square_root(last)
+            store(gates, "m")
+            store(cell, "c")
+            store(done, "h")
+
+            project_rows(ahead, G_F, "c", "f_sum")
+            project_rows(ahead, G_I, "c", "i_sum")
+            project_cols(ahead, G_K, "c", "k", ACT.Identity, bk_scaled[:], k_scale)
+            to_rows(cell, "q")

@@ -21,6 +21,7 @@ CHUNKS = TILES // TPC
 CW = TPC * H
 GATES = 6
 G_I, G_F, G_K, G_Q, G_V, G_O = 0, 1, 2, 3, 4, 5
+W_NI = GATES
 FLOPS = 2 * ROWS * K * H * GATES
 
 
@@ -81,7 +82,7 @@ def tile_mlstmblock_pb_t_kernel(
         name="quant", bufs=2
     ) as quant, tc.tile_pool(name="work", bufs=2) as work, tc.tile_pool(
         name="outs", bufs=3
-    ) as outs, tc.psum_pool(name="front", bufs=3) as front, tc.psum_pool(
+    ) as outs, tc.psum_pool(name="front", bufs=4) as front, tc.psum_pool(
         name="gate", bufs=1
     ) as gate, tc.psum_pool(name="rows", bufs=3) as rows, tc.manual_schedule():
         kept = {}
@@ -174,9 +175,9 @@ def tile_mlstmblock_pb_t_kernel(
                 stop=True,
             )
 
-        w_grouped = const.tile([P, GATES, H, 4], BF16, align_bytes=64)
-        w_codes = const.tile([P, GATES * H], U32, align_bytes=64)
-        w_scales = const.tile([P, GATES * H], U8, align_bytes=64)
+        w_grouped = const.tile([P, GATES + 1, H, 4], BF16, align_bytes=64)
+        w_codes = const.tile([P, (GATES + 1) * H], U32, align_bytes=64)
+        w_scales = const.tile([P, (GATES + 1) * H], U8, align_bytes=64)
 
         def quantise_weights(g0, g1):
             nc.vector.tensor_copy(
@@ -189,6 +190,14 @@ def tile_mlstmblock_pb_t_kernel(
             )
 
         quantise_weights(G_I, G_F + 1)
+        nc.vector.tensor_scalar_mul(
+            out=w_grouped[:, W_NI], in0=w_raw[:, G_I].rearrange("p t c -> p c t"), scalar1=-1.0
+        )
+        nc.vector.quantize_mx(
+            out=w_codes[:, W_NI * H :].bitcast(FP8X4),
+            scales=w_scales[:, W_NI * H :],
+            in_=w_grouped[:, W_NI].rearrange("p c t -> p (c t)"),
+        )
         bias_col = const.tile([P, GATES], F32)
         nc.vector.tensor_copy(out=bias_col[:], in_=spread[:, 0:GATES])
         bk_scaled = const.tile([P, 1], F32)
@@ -255,21 +264,22 @@ def tile_mlstmblock_pb_t_kernel(
             )
             kept[("mx" + nm, c)] = (codes, scales)
 
-        def project_rows(c, g, nm, name):
+        def project_rows(c, planes, nm, name):
             if absent(c):
                 return
             codes, scales = kept[("mx" + nm, c)]
             acc = gate.tile([P, CW], F32, tag=name, name=name)
             for t in range(TPC):
-                nc.tensor.matmul_mx(
-                    out=acc[:, t * H : (t + 1) * H],
-                    lhsT=codes[:, t * P : (t + 1) * P].bitcast(FP8X4),
-                    lhsT_scale=scales[:, t * P : (t + 1) * P],
-                    rhs=w_codes[:, g * H : (g + 1) * H].bitcast(FP8X4),
-                    rhs_scale=w_scales[:, g * H : (g + 1) * H],
-                    start=True,
-                    stop=True,
-                )
+                for n, g in enumerate(planes):
+                    nc.tensor.matmul_mx(
+                        out=acc[:, t * H : (t + 1) * H],
+                        lhsT=codes[:, t * P : (t + 1) * P].bitcast(FP8X4),
+                        lhsT_scale=scales[:, t * P : (t + 1) * P],
+                        rhs=w_codes[:, g * H : (g + 1) * H].bitcast(FP8X4),
+                        rhs_scale=w_scales[:, g * H : (g + 1) * H],
+                        start=n == 0,
+                        stop=n == len(planes) - 1,
+                    )
             kept[(name, c)] = acc
 
         def project_cols(c, g, nm, name, func, bias_ap, scale):
@@ -320,13 +330,6 @@ def tile_mlstmblock_pb_t_kernel(
                 in1=kept[(b, c)][:],
                 op0=op0,
                 op1=op1,
-            )
-
-        def add_row(pool, out_name, c, a, row):
-            if absent(c):
-                return
-            nc.gpsimd.tensor_tensor(
-                out=by_tile(new(pool, out_name, c)[:]), in0=by_tile(kept[(a, c)][:]), in1=over_tiles(row), op=ALU.add
             )
 
         def exponential(c, out_name, sign):
@@ -382,12 +385,12 @@ def tile_mlstmblock_pb_t_kernel(
         for j in range(-2, CHUNKS + 2):
             ahead, gates, cell, last, done = j + 2, j + 1, j, j - 1, j - 2
 
-            tensor_tensor(nc.vector, work, "u", gates, "f_sum", "m_shifted", ALU.add)
+            tensor_tensor(nc.vector, work, "d", gates, "d_sum", "m_shifted", ALU.add)
             scalar_then_tensor(work, "ik", cell, "exp_minus_d", 1.0, ALU.min, "k", ALU.mult)
-            tensor_tensor(nc.vector, work, "d", gates, "u", "i_sum", ALU.subtract)
             scalar_then_tensor(work, "fn", cell, "exp_d", 1.0, ALU.min, "n_prev", ALU.mult)
             tensor_tensor(nc.vector, work, "nq", last, "q", "n_t", ALU.mult)
             leave_psum(gates, "k")
+            leave_psum(gates, "i")
             to_rows(cell, "v")
             tensor_tensor(nc.gpsimd, outs, "n_t", cell, "fn", "ik", ALU.add)
 
@@ -401,10 +404,8 @@ def tile_mlstmblock_pb_t_kernel(
             store(cell, "n")
 
             tensor_tensor(nc.vector, work, "ikv", cell, "v", "ik", ALU.mult)
-            scalar_then_tensor(work, "m_less_bi", gates, "d", 0.0, ALU.max, "i_sum", ALU.add)
             scalar_then_tensor(work, "fc", cell, "exp_d", 1.0, ALU.min, "c_prev", ALU.mult)
             tensor_tensor(nc.vector, work, "cq", last, "q", "c_t", ALU.mult)
-            add_row(outs, "m_t", gates, "m_less_bi", bi_row)
             tensor_tensor(nc.gpsimd, outs, "c_t", cell, "fc", "ikv", ALU.add)
 
             to_rows(last, "o")
@@ -414,12 +415,14 @@ def tile_mlstmblock_pb_t_kernel(
             leave_psum(gates, "o")
             project_cols(gates, G_Q, "c", "q", ACT.Identity, bias_col[:, G_Q : G_Q + 1], 1.0)
             leave_psum(gates, "q")
+            to_rows(gates, "i")
             to_rows(gates, "k")
 
             quantise_x(ahead, "c")
             add_epsilon(done)
             scalar_then_tensor(work, "h_unscaled", last, "o", 1.0, ALU.add, "cq", ALU.mult)
             reciprocal(done)
+            scalar_then_tensor(outs, "m_t", gates, "d", 0.0, ALU.max, "i", ALU.add)
             quantise_x(ahead, "l")
             scale_rows(done)
             sum_of_squares(last)
@@ -430,7 +433,7 @@ def tile_mlstmblock_pb_t_kernel(
             store(cell, "c")
             store(done, "h")
 
-            project_rows(ahead, G_F, "c", "f_sum")
-            project_rows(ahead, G_I, "c", "i_sum")
+            project_rows(ahead, (G_F, W_NI), "c", "d_sum")
+            project_cols(ahead, G_I, "c", "i", ACT.Identity, bias_col[:, G_I : G_I + 1], 1.0)
             project_cols(ahead, G_K, "c", "k", ACT.Identity, bk_scaled[:], k_scale)
             to_rows(cell, "q")

@@ -16,13 +16,13 @@ ROWS = 4096
 K = 512
 H = 128
 TILES = ROWS // P
-TPC = 4
-CHUNKS = TILES // TPC
-CW = TPC * H
-GATES = 6
-G_I, G_F, G_K, G_Q, G_V, G_O = 0, 1, 2, 3, 4, 5
-W_NI = GATES
-FLOPS = 2 * ROWS * K * H * GATES
+SIZES = (4, 4, 4, 4, 4, 4, 4, 4)
+CHUNKS = len(SIZES)
+FIRST = tuple(sum(SIZES[:c]) for c in range(CHUNKS))
+CW = 4 * H
+B_I, B_F, B_K, B_Q, B_V, B_O = range(6)
+W_F, W_NI, W_I, W_K, W_Q, W_V, W_O = range(7)
+FLOPS = 2 * ROWS * K * H * 6
 
 
 def tile_mlstmblock_pb_t_kernel(
@@ -56,35 +56,16 @@ def tile_mlstmblock_pb_t_kernel(
         return dram.rearrange("(p t) w -> p t w", t=TILES)
 
     x_views = {"c": by_partition(x_conv), "l": by_partition(x_left)}
-    state_views = {"m": by_partition(m_prev), "n": by_partition(n_prev), "c": by_partition(c_prev)}
-    out_views = {
-        "h": by_partition(out_0),
-        "c": by_partition(out_1),
-        "n": by_partition(out_2),
-        "m": by_partition(out_3),
-    }
-    weights = [None] * GATES
-    biases = [None] * GATES
-    for g, w_ap, b_ap in (
-        (G_I, wi_w, wi_b),
-        (G_F, wf_w, wf_b),
-        (G_K, wk_w[0], wk_b),
-        (G_Q, wq_w[0], wq_b),
-        (G_V, wv_w[0], wv_b),
-        (G_O, wo_w, wo_b),
-    ):
-        weights[g] = w_ap
-        biases[g] = b_ap
+    m_view, n_view, c_view = by_partition(m_prev), by_partition(n_prev), by_partition(c_prev)
+    out_views = {"h": by_partition(out_0), "c": by_partition(out_1), "n": by_partition(out_2), "m": by_partition(out_3)}
 
-    with tc.tile_pool(name="const", bufs=1) as const, tc.tile_pool(
-        name="xin", bufs=3
-    ) as xin, tc.tile_pool(name="state", bufs=CHUNKS // 2) as state, tc.tile_pool(
-        name="quant", bufs=2
-    ) as quant, tc.tile_pool(name="work", bufs=2) as work, tc.tile_pool(
+    with tc.tile_pool(name="const", bufs=1) as const, tc.tile_pool(name="xin", bufs=4) as xin, tc.tile_pool(
+        name="states", bufs=1
+    ) as states, tc.tile_pool(name="quant", bufs=2) as quant, tc.tile_pool(name="work", bufs=3) as work, tc.tile_pool(
         name="outs", bufs=3
     ) as outs, tc.psum_pool(name="front", bufs=4) as front, tc.psum_pool(
-        name="gate", bufs=1
-    ) as gate, tc.psum_pool(name="rows", bufs=3) as rows, tc.manual_schedule():
+        name="dsum", bufs=1
+    ) as dsum, tc.psum_pool(name="rows", bufs=3) as rows, tc.manual_schedule():
         kept = {}
 
         def absent(c):
@@ -94,140 +75,95 @@ def tile_mlstmblock_pb_t_kernel(
             return ap.rearrange("p (t h) -> p t h", h=H)
 
         def new(pool, name, c):
-            kept[(name, c)] = pool.tile([P, CW], F32, tag=name, name=name)
+            kept[(name, c)] = pool.tile([P, SIZES[c] * H], F32, tag=name, name=name)
             return kept[(name, c)]
+
+        def tiles(c):
+            return slice(FIRST[c], FIRST[c] + SIZES[c])
+
+        def cols(c):
+            return slice(FIRST[c] * H, (FIRST[c] + SIZES[c]) * H)
 
         def load_x(c, nm):
             if absent(c):
                 return
-            x_sb = xin.tile([P, TPC * K], BF16, tag="x" + nm, name="x" + nm)
-            nc.sync.dma_start(
-                out=x_sb[:].rearrange("p (t k) -> p t k", t=TPC),
-                in_=x_views[nm][:, c * TPC : (c + 1) * TPC, :],
-            )
+            x_sb = xin.tile([P, SIZES[c] * K], BF16, tag="x" + nm, name="x" + nm)
+            nc.sync.dma_start(out=x_sb[:].rearrange("p (t k) -> p t k", k=K), in_=x_views[nm][:, tiles(c), :])
             kept[("x" + nm, c)] = x_sb
 
-        def load_state(c):
-            if absent(c) or c % 2 == 1:
-                return
-            for nm in ("n", "c"):
-                st = state.tile([P, 2 * CW], BF16, tag="st" + nm, name="st" + nm)
-                nc.sync.dma_start(out=by_tile(st[:]), in_=state_views[nm][:, c * TPC : (c + 2) * TPC, :])
-                kept[(nm + "_prev", c)] = st[:, 0:CW]
-                kept[(nm + "_prev", c + 1)] = st[:, CW : 2 * CW]
+        m_all = const.tile([P, TILES * H], BF16)
 
-        m_all = const.tile([P, CHUNKS * CW], BF16)
+        def load_state(c, count):
+            w = sum(SIZES[c : c + count]) * H
+            for nm, view in (("n", n_view), ("c", c_view)):
+                st = states.tile([P, w], BF16, tag="%s%d" % (nm, c), name="%s%d" % (nm, c))
+                nc.sync.dma_start(out=by_tile(st[:]), in_=view[:, FIRST[c] : FIRST[c] + w // H, :])
+                for i in range(c, c + count):
+                    kept[(nm + "_prev", i)] = st[:, (FIRST[i] - FIRST[c]) * H : (FIRST[i] - FIRST[c] + SIZES[i]) * H]
 
-        def load_m(first, count):
-            nc.sync.dma_start(
-                out=by_tile(m_all[:, first * CW : (first + count) * CW]),
-                in_=state_views["m"][:, first * TPC : (first + count) * TPC, :],
-            )
+        def load_m(t0, t1):
+            nc.sync.dma_start(out=by_tile(m_all[:, t0 * H : t1 * H]), in_=m_view[:, t0:t1, :])
 
         def store(c, nm):
             if absent(c):
                 return
             nc.sync.dma_start(
-                out=out_views[nm][:, c * TPC : (c + 1) * TPC, :], in_=by_tile(kept[(nm + "_t", c)][:])
+                out=out_views[nm][:, tiles(c), :], in_=by_tile(kept[(nm + "_t", c)][:])
             )
 
         load_x(0, "c")
         bias_rows = const.tile([P, P], BF16)
         nc.vector.memset(bias_rows[:], 0.0)
-        for g in range(GATES):
-            nc.sync.dma_start(out=bias_rows[g : g + 1, :], in_=biases[g].unsqueeze(0))
-        w_raw = const.tile([P, GATES, 4, H], BF16)
-        for g in range(GATES):
-            nc.sync.dma_start(
-                out=w_raw[:, g, :, :],
-                in_=weights[g].rearrange("(q j) c -> q j c", j=4),
-            )
-        load_x(0, "l")
-        load_m(0, CHUNKS // 2)
-        load_state(0)
+        for b, b_ap in ((B_I, wi_b), (B_F, wf_b), (B_K, wk_b), (B_Q, wq_b), (B_V, wv_b), (B_O, wo_b)):
+            nc.sync.dma_start(out=bias_rows[b : b + 1, :], in_=b_ap.unsqueeze(0))
+        w_raw = const.tile([P, 6, 4, H], BF16)
+        for g, w_ap in enumerate((wf_w, wi_w, wk_w[0], wq_w[0], wv_w[0], wo_w)):
+            nc.sync.dma_start(out=w_raw[:, g, :, :], in_=w_ap.rearrange("(q j) c -> q j c", j=4))
+            if g == 1:
+                load_x(0, "l")
+                load_m(0, 4)
+        load_m(4, 8)
         load_x(1, "c")
         load_x(1, "l")
-        load_m(CHUNKS // 2, CHUNKS // 2)
+        load_state(0, 1)
         load_x(2, "c")
         load_x(2, "l")
+        load_m(8, TILES)
+        load_state(1, 1)
+        load_x(3, "c")
+        load_x(3, "l")
+        for c in range(2, CHUNKS):
+            load_state(c, 1)
 
         zero = const.tile([P, 1], F32)
         nc.vector.memset(zero[:], 0.0)
         one = const.tile([P, 1], F32)
         nc.scalar.activation(out=one[:], in_=zero[:], func=ACT.Exp)
-        half = const.tile([P, TPC], F32)
+        half = const.tile([P, 4], F32)
         nc.vector.memset(half[:], 0.5)
         ident = const.tile([P, P], F32)
         make_identity(nc, ident[:])
         ident_bf = const.tile([P, P], BF16)
         nc.vector.tensor_copy(out=ident_bf[:], in_=ident[:])
-
         bias_f32 = const.tile([P, P], F32)
         nc.vector.tensor_copy(out=bias_f32[:], in_=bias_rows[:])
-        spread = rows.tile([P, CW], F32, tag="rows", name="spread")
-        nc.tensor.transpose(spread[:, 0:P], bias_f32[:], ident[:])
-        for g in (G_I, G_F):
-            nc.tensor.matmul(
-                out=spread[:, (g + 1) * P : (g + 2) * P],
-                lhsT=ident_bf[:, g : g + 1].to_broadcast([P, P]),
-                rhs=bias_rows[:],
-                start=True,
-                stop=True,
-            )
 
-        w_grouped = const.tile([P, GATES + 1, H, 4], BF16, align_bytes=64)
-        w_codes = const.tile([P, (GATES + 1) * H], U32, align_bytes=64)
-        w_scales = const.tile([P, (GATES + 1) * H], U8, align_bytes=64)
+        w_grouped = const.tile([P, 7, H, 4], BF16, align_bytes=64)
+        w_codes = const.tile([P, 7 * H], U32, align_bytes=64)
+        w_scales = const.tile([P, 7 * H], U8, align_bytes=64)
+
+        def group_weights(out_g, raw_g):
+            nc.vector.tensor_copy(out=w_grouped[:, out_g], in_=w_raw[:, raw_g].rearrange("p j c -> p c j"))
 
         def quantise_weights(g0, g1):
-            nc.vector.tensor_copy(
-                out=w_grouped[:, g0:g1], in_=w_raw[:, g0:g1].rearrange("p g t c -> p g c t")
-            )
             nc.vector.quantize_mx(
                 out=w_codes[:, g0 * H : g1 * H].bitcast(FP8X4),
                 scales=w_scales[:, g0 * H : g1 * H],
                 in_=w_grouped[:, g0:g1].rearrange("p g c t -> p (g c t)"),
             )
 
-        quantise_weights(G_I, G_F + 1)
-        nc.vector.tensor_scalar_mul(
-            out=w_grouped[:, W_NI], in0=w_raw[:, G_I].rearrange("p t c -> p c t"), scalar1=-1.0
-        )
-        nc.vector.quantize_mx(
-            out=w_codes[:, W_NI * H :].bitcast(FP8X4),
-            scales=w_scales[:, W_NI * H :],
-            in_=w_grouped[:, W_NI].rearrange("p c t -> p (c t)"),
-        )
-        bias_col = const.tile([P, GATES], F32)
-        nc.vector.tensor_copy(out=bias_col[:], in_=spread[:, 0:GATES])
-        bk_scaled = const.tile([P, 1], F32)
-        nc.vector.tensor_scalar_mul(out=bk_scaled[:], in0=bias_col[:, G_K : G_K + 1], scalar1=k_scale)
-        bo_half = const.tile([P, 1], F32)
-        nc.vector.tensor_scalar_mul(out=bo_half[:], in0=bias_col[:, G_O : G_O + 1], scalar1=0.5)
-        bi_row = const.tile([P, H], F32)
-        nc.vector.tensor_copy(out=bi_row[:], in_=spread[:, (G_I + 1) * P : (G_I + 2) * P])
-        bf_minus_bi_row = const.tile([P, H], F32)
-        nc.vector.tensor_tensor(
-            out=bf_minus_bi_row[:], in0=spread[:, (G_F + 1) * P : (G_F + 2) * P], in1=bi_row[:], op=ALU.subtract
-        )
-        quantise_weights(G_K, G_Q + 1)
-        quantise_weights(G_V, G_O + 1)
-
-        def over_tiles(row):
-            return row[:].unsqueeze(1).to_broadcast([P, TPC, H])
-
-        m_shifted = const.tile([P, CHUNKS * CW], F32)
-        for c in range(CHUNKS):
-            nc.gpsimd.tensor_tensor(
-                out=by_tile(m_shifted[:, c * CW : (c + 1) * CW]),
-                in0=by_tile(m_all[:, c * CW : (c + 1) * CW]),
-                in1=over_tiles(bf_minus_bi_row),
-                op=ALU.add,
-            )
-            kept[("m_shifted", c)] = m_shifted[:, c * CW : (c + 1) * CW]
-
         def transpose_x(c, nm, half_no):
-            if absent(c):
+            if absent(c) or 2 * half_no >= SIZES[c]:
                 return
             words = kept[("x" + nm, c)][:].bitcast(F32)
             bank = front.tile([P, CW], F32, tag="front", name="xT")
@@ -242,11 +178,11 @@ def tile_mlstmblock_pb_t_kernel(
             kept[("xT" + nm, c, half_no)] = bank
 
         def regroup_x(c, nm, half_no):
-            if absent(c):
+            if absent(c) or 2 * half_no >= SIZES[c]:
                 return
             if half_no == 0:
                 kept[("grouped" + nm, c)] = quant.tile(
-                    [P, 4 * CW], BF16, tag="grouped" + nm, name="grouped" + nm, align_bytes=64
+                    [P, SIZES[c] * K], BF16, tag="grouped" + nm, name="grouped" + nm, align_bytes=64
                 )
             words = kept[("grouped" + nm, c)][:].bitcast(F32)
             nc.scalar.copy(
@@ -257,92 +193,147 @@ def tile_mlstmblock_pb_t_kernel(
         def quantise_x(c, nm):
             if absent(c):
                 return
-            codes = quant.tile([P, CW], U32, tag="codes" + nm, name="codes" + nm, align_bytes=64)
-            scales = quant.tile([P, CW], U8, tag="scales" + nm, name="scales" + nm, align_bytes=64)
+            codes = quant.tile([P, SIZES[c] * H], U32, tag="codes" + nm, name="codes" + nm, align_bytes=64)
+            scales = quant.tile([P, SIZES[c] * H], U8, tag="scales" + nm, name="scales" + nm, align_bytes=64)
             nc.vector.quantize_mx(
                 out=codes[:].bitcast(FP8X4), scales=scales[:], in_=kept[("grouped" + nm, c)][:]
             )
             kept[("mx" + nm, c)] = (codes, scales)
 
-        def project_rows(c, planes, nm, name):
-            if absent(c):
-                return
-            codes, scales = kept[("mx" + nm, c)]
-            acc = gate.tile([P, CW], F32, tag=name, name=name)
-            for t in range(TPC):
-                for n, g in enumerate(planes):
-                    nc.tensor.matmul_mx(
-                        out=acc[:, t * H : (t + 1) * H],
-                        lhsT=codes[:, t * P : (t + 1) * P].bitcast(FP8X4),
-                        lhsT_scale=scales[:, t * P : (t + 1) * P],
-                        rhs=w_codes[:, g * H : (g + 1) * H].bitcast(FP8X4),
-                        rhs_scale=w_scales[:, g * H : (g + 1) * H],
-                        start=n == 0,
-                        stop=n == len(planes) - 1,
-                    )
-            kept[(name, c)] = acc
-
-        def project_cols(c, g, nm, name, func, bias_ap, scale):
-            if absent(c):
-                return
-            codes, scales = kept[("mx" + nm, c)]
-            acc = front.tile([P, CW], F32, tag="front", name="acc")
+        def matmul_mx(out, lhs, rhs, first, last):
             nc.tensor.matmul_mx(
-                out=acc[:],
-                lhsT=w_codes[:, g * H : (g + 1) * H].bitcast(FP8X4),
-                lhsT_scale=w_scales[:, g * H : (g + 1) * H],
-                rhs=codes[:].bitcast(FP8X4),
-                rhs_scale=scales[:],
-                start=True,
-                stop=True,
+                out=out,
+                lhsT=lhs[0].bitcast(FP8X4),
+                lhsT_scale=lhs[1],
+                rhs=rhs[0].bitcast(FP8X4),
+                rhs_scale=rhs[1],
+                start=first,
+                stop=last,
             )
-            kept[("acc" + name, c)] = (acc, func, bias_ap, scale)
 
-        def leave_psum(c, name):
+        def weight(g):
+            return w_codes[:, g * H : (g + 1) * H], w_scales[:, g * H : (g + 1) * H]
+
+        def project_d(c):
             if absent(c):
                 return
-            acc, func, bias_ap, scale = kept[("acc" + name, c)]
+            codes, scales = kept[("mxc", c)]
+            acc = dsum.tile([P, SIZES[c] * H], F32, tag="d_sum", name="d_sum")
+            for t in range(SIZES[c]):
+                x_tile = codes[:, t * P : (t + 1) * P], scales[:, t * P : (t + 1) * P]
+                out = acc[:, t * H : (t + 1) * H]
+                matmul_mx(out, x_tile, weight(W_F), True, False)
+                matmul_mx(out, x_tile, weight(W_NI), False, True)
+            kept[("d_sum", c)] = acc
+
+        def project(c, name):
+            if absent(c):
+                return
+            g, nm = {"i": (W_I, "c"), "k": (W_K, "c"), "q": (W_Q, "c"), "v": (W_V, "l"), "o": (W_O, "l")}[name]
+            codes, scales = kept[("mx" + nm, c)]
+            acc = front.tile([P, SIZES[c] * H], F32, tag="front", name="acc")
+            matmul_mx(acc[:], weight(g), (codes[:], scales[:]), True, True)
+            kept[("acc_" + name, c)] = acc
+
+        def leave(c, name):
+            if absent(c):
+                return
+            func, bias, scale = {
+                "i": (ACT.Identity, bias_col[:, B_I : B_I + 1], 1.0),
+                "k": (ACT.Identity, bk_scaled[:], k_scale),
+                "q": (ACT.Identity, bias_col[:, B_Q : B_Q + 1], 1.0),
+                "v": (ACT.Identity, bias_col[:, B_V : B_V + 1], 1.0),
+                "o": (ACT.Tanh, bo_half[:], 0.5),
+            }[name]
             nc.scalar.activation(
-                out=new(work, name + "_cols", c)[:], in_=acc[:], func=func, bias=bias_ap, scale=scale
+                out=new(work, name + "_cols", c)[:], in_=kept[("acc_" + name, c)][:], func=func, bias=bias, scale=scale
             )
 
         def to_rows(c, name):
             if absent(c):
                 return
             src = kept[(name + "_cols", c)]
-            bank = rows.tile([P, CW], F32, tag="rows", name=name + "_rows")
-            for t in range(TPC):
+            bank = rows.tile([P, SIZES[c] * H], F32, tag="rows", name=name + "_rows")
+            for t in range(SIZES[c]):
                 nc.tensor.transpose(bank[:, t * H : (t + 1) * H], src[:, t * P : (t + 1) * P], ident[:])
             kept[(name, c)] = bank
 
-        def tensor_tensor(engine, pool, out_name, c, a, b, op):
+        m_shifted = const.tile([P, TILES * H], F32)
+
+        def shift_m(c, engine):
+            if absent(c):
+                return
+            engine.tensor_tensor(
+                out=by_tile(m_shifted[:, cols(c)]),
+                in0=by_tile(m_all[:, cols(c)]),
+                in1=bf_minus_bi[:].unsqueeze(1).to_broadcast([P, SIZES[c], H]),
+                op=ALU.add,
+            )
+            kept[("m_shifted", c)] = m_shifted[:, cols(c)]
+
+        def two(engine, pool, out_name, c, a, b, op):
             if absent(c):
                 return
             engine.tensor_tensor(out=new(pool, out_name, c)[:], in0=kept[(a, c)][:], in1=kept[(b, c)][:], op=op)
 
-        def scalar_then_tensor(pool, out_name, c, a, scalar, op0, b, op1):
+        def three(pool, out_name, c, a, scalar, op0, b, op1):
             if absent(c):
                 return
             nc.vector.scalar_tensor_tensor(
-                out=new(pool, out_name, c)[:],
-                in0=kept[(a, c)][:],
-                scalar=scalar,
-                in1=kept[(b, c)][:],
-                op0=op0,
-                op1=op1,
+                out=new(pool, out_name, c)[:], in0=kept[(a, c)][:], scalar=scalar, in1=kept[(b, c)][:], op0=op0, op1=op1
             )
+
+        def d_new(c):
+            two(nc.vector, work, "d", c, "d_sum", "m_shifted", ALU.add)
+
+        def m_new(c):
+            three(outs, "m_t", c, "d", 0.0, ALU.max, "i", ALU.add)
+            store(c, "m")
+
+        def ik(c):
+            three(work, "ik", c, "ei", 1.0, ALU.min, "k", ALU.mult)
+
+        def fn(c):
+            three(work, "fn", c, "ef", 1.0, ALU.min, "n_prev", ALU.mult)
+
+        def fc(c):
+            three(work, "fc", c, "ef", 1.0, ALU.min, "c_prev", ALU.mult)
+
+        def ikv(c):
+            two(nc.vector, work, "ikv", c, "v", "ik", ALU.mult)
+
+        def n_new(c, engine):
+            two(engine, outs, "n_t", c, "fn", "ik", ALU.add)
+            store(c, "n")
+
+        def c_new(c, engine):
+            two(engine, outs, "c_t", c, "fc", "ikv", ALU.add)
+            store(c, "c")
+
+        def nq(c):
+            two(nc.vector, work, "nq", c, "q", "n_t", ALU.mult)
+
+        def cq(c):
+            two(nc.vector, work, "cq", c, "q", "c_t", ALU.mult)
+
+        def ho(c):
+            three(work, "ho", c, "o", 1.0, ALU.add, "cq", ALU.mult)
 
         def exponential(c, out_name, sign):
             if absent(c):
                 return
             nc.scalar.activation(out=new(work, out_name, c)[:], in_=kept[("d", c)][:], func=ACT.Exp, scale=sign)
 
+        def small(c, name):
+            kept[(name, c)] = work.tile([P, SIZES[c]], F32, tag=name, name=name)
+            return kept[(name, c)]
+
         def sum_of_squares(c):
             if absent(c):
                 return
-            squares = work.tile([P, CW], F32, tag="squares", name="squares")
-            ss = work.tile([P, TPC], F32, tag="ss", name="ss")
-            for t in range(TPC):
+            squares = work.tile([P, SIZES[c] * H], F32, tag="squares", name="squares")
+            ss = small(c, "ss")
+            for t in range(SIZES[c]):
                 nc.scalar.activation(
                     out=squares[:, t * H : (t + 1) * H],
                     in_=kept[("nq", c)][:, t * H : (t + 1) * H],
@@ -350,16 +341,13 @@ def tile_mlstmblock_pb_t_kernel(
                     scale=2.0,
                     accum_out=ss[:, t : t + 1],
                 )
-            kept[("ss", c)] = ss
-
-        def small(c, name):
-            kept[(name, c)] = work.tile([P, TPC], F32, tag=name, name=name)
-            return kept[(name, c)]
 
         def square_root(c):
             if absent(c):
                 return
-            nc.gpsimd.tensor_tensor(out=small(c, "root")[:], in0=kept[("ss", c)][:], in1=half[:], op=ALU.pow)
+            nc.gpsimd.tensor_tensor(
+                out=small(c, "root")[:], in0=kept[("ss", c)][:], in1=half[:, 0 : SIZES[c]], op=ALU.pow
+            )
 
         def add_epsilon(c):
             if absent(c):
@@ -375,65 +363,95 @@ def tile_mlstmblock_pb_t_kernel(
             if absent(c):
                 return
             h_t = new(outs, "h_t", c)
-            for t in range(TPC):
+            for t in range(SIZES[c]):
                 nc.vector.tensor_scalar_mul(
                     out=h_t[:, t * H : (t + 1) * H],
-                    in0=kept[("h_unscaled", c)][:, t * H : (t + 1) * H],
+                    in0=kept[("ho", c)][:, t * H : (t + 1) * H],
                     scalar1=kept[("scale", c)][:, t : t + 1],
                 )
+            store(c, "h")
+
+        spread = rows.tile([P, CW], F32, tag="rows", name="spread")
+        nc.tensor.transpose(spread[:, 0:P], bias_f32[:], ident[:])
+        for n, b in enumerate((B_I, B_F)):
+            nc.tensor.matmul(
+                out=spread[:, (n + 1) * P : (n + 2) * P],
+                lhsT=ident_bf[:, b : b + 1].to_broadcast([P, P]),
+                rhs=bias_rows[:],
+                start=True,
+                stop=True,
+            )
+        bias_col = const.tile([P, 6], F32)
+        nc.vector.tensor_copy(out=bias_col[:], in_=spread[:, 0:6])
+        bi_row = const.tile([P, H], F32)
+        nc.vector.tensor_copy(out=bi_row[:], in_=spread[:, P : 2 * P])
+        bo_half = const.tile([P, 1], F32)
+        nc.vector.tensor_scalar_mul(out=bo_half[:], in0=bias_col[:, B_O : B_O + 1], scalar1=0.5)
+        bk_scaled = const.tile([P, 1], F32)
+        nc.vector.tensor_scalar_mul(out=bk_scaled[:], in0=bias_col[:, B_K : B_K + 1], scalar1=k_scale)
+        bf_minus_bi = const.tile([P, H], F32)
+        nc.vector.tensor_tensor(out=bf_minus_bi[:], in0=spread[:, 2 * P : 3 * P], in1=bi_row[:], op=ALU.subtract)
+
+        def prepare_x(c, nm, half_no):
+            transpose_x(c, nm, half_no)
+            regroup_x(c, nm, half_no)
+
+        group_weights(W_F, 0)
+        nc.vector.tensor_scalar_mul(out=w_grouped[:, W_NI], in0=w_raw[:, 1].rearrange("p j c -> p c j"), scalar1=-1.0)
+        quantise_weights(W_F, W_NI + 1)
 
         for j in range(-2, CHUNKS + 2):
             ahead, gates, cell, last, done = j + 2, j + 1, j, j - 1, j - 2
 
-            tensor_tensor(nc.vector, work, "d", gates, "d_sum", "m_shifted", ALU.add)
-            scalar_then_tensor(work, "ik", cell, "exp_minus_d", 1.0, ALU.min, "k", ALU.mult)
-            scalar_then_tensor(work, "fn", cell, "exp_d", 1.0, ALU.min, "n_prev", ALU.mult)
-            tensor_tensor(nc.vector, work, "nq", last, "q", "n_t", ALU.mult)
-            leave_psum(gates, "k")
-            leave_psum(gates, "i")
+            ik(cell)
+            fn(cell)
+            nq(last)
+            leave(gates, "i")
             to_rows(cell, "v")
-            tensor_tensor(nc.gpsimd, outs, "n_t", cell, "fn", "ik", ALU.add)
-
+            n_new(cell, nc.gpsimd)
             for nm in ("c", "l"):
                 for half_no in range(2):
-                    transpose_x(ahead, nm, half_no)
-                    regroup_x(ahead, nm, half_no)
-            load_x(j + 5, "c")
-            load_x(j + 5, "l")
-            load_state(j + 4)
-            store(cell, "n")
-
-            tensor_tensor(nc.vector, work, "ikv", cell, "v", "ik", ALU.mult)
-            scalar_then_tensor(work, "fc", cell, "exp_d", 1.0, ALU.min, "c_prev", ALU.mult)
-            tensor_tensor(nc.vector, work, "cq", last, "q", "c_t", ALU.mult)
-            tensor_tensor(nc.gpsimd, outs, "c_t", cell, "fc", "ikv", ALU.add)
-
+                    prepare_x(ahead, nm, half_no)
+            sum_of_squares(last)
+            leave(gates, "k")
+            load_x(j + 6, "c")
+            load_x(j + 6, "l")
+            ikv(cell)
+            fc(cell)
+            cq(last)
+            d_new(gates)
+            c_new(cell, nc.gpsimd)
             to_rows(last, "o")
-            project_cols(gates, G_V, "l", "v", ACT.Identity, bias_col[:, G_V : G_V + 1], 1.0)
-            leave_psum(gates, "v")
-            project_cols(gates, G_O, "l", "o", ACT.Tanh, bo_half[:], 0.5)
-            leave_psum(gates, "o")
-            project_cols(gates, G_Q, "c", "q", ACT.Identity, bias_col[:, G_Q : G_Q + 1], 1.0)
-            leave_psum(gates, "q")
+            for name in ("v", "o", "q"):
+                project(gates, name)
+                leave(gates, name)
             to_rows(gates, "i")
             to_rows(gates, "k")
-
             quantise_x(ahead, "c")
+            if j == -2:
+                nc.scalar.copy(out=w_grouped[:, W_I], in_=w_raw[:, 1].rearrange("p j c -> p c j"))
+                group_weights(W_K, 2)
+                quantise_weights(W_I, W_K + 1)
+                shift_m(0, nc.vector)
+                shift_m(1, nc.gpsimd)
             add_epsilon(done)
-            scalar_then_tensor(work, "h_unscaled", last, "o", 1.0, ALU.add, "cq", ALU.mult)
+            ho(last)
             reciprocal(done)
-            scalar_then_tensor(outs, "m_t", gates, "d", 0.0, ALU.max, "i", ALU.add)
+            m_new(gates)
             quantise_x(ahead, "l")
+            if j == -2:
+                for g_no, raw_no in ((W_Q, 3), (W_V, 4)):
+                    nc.scalar.copy(out=w_grouped[:, g_no], in_=w_raw[:, raw_no].rearrange("p j c -> p c j"))
+                group_weights(W_O, 5)
+                quantise_weights(W_Q, W_Q + 1)
+                quantise_weights(W_V, W_O + 1)
             scale_rows(done)
-            sum_of_squares(last)
-            exponential(gates, "exp_minus_d", -1.0)
-            exponential(gates, "exp_d", 1.0)
+            exponential(gates, "ei", -1.0)
+            exponential(gates, "ef", 1.0)
             square_root(last)
-            store(gates, "m")
-            store(cell, "c")
-            store(done, "h")
-
-            project_rows(ahead, (G_F, W_NI), "c", "d_sum")
-            project_cols(ahead, G_I, "c", "i", ACT.Identity, bias_col[:, G_I : G_I + 1], 1.0)
-            project_cols(ahead, G_K, "c", "k", ACT.Identity, bk_scaled[:], k_scale)
+            if j >= -1:
+                shift_m(j + 3, nc.gpsimd)
+            project_d(ahead)
+            project(ahead, "i")
+            project(ahead, "k")
             to_rows(cell, "q")

@@ -122,9 +122,9 @@ def tile_mlstmblock_pb_t_kernel(
             if g == 1:
                 load_x(0, "l")
                 load_m(0, 4)
-        load_m(4, 8)
         load_x(1, "c")
         load_x(1, "l")
+        load_m(4, 8)
         load_state(0, 1)
         load_x(2, "c")
         load_x(2, "l")
@@ -371,6 +371,11 @@ def tile_mlstmblock_pb_t_kernel(
                 )
             store(c, "h")
 
+        warm = rows.tile([P, CW], F32, tag="rows", name="warm")
+        for n in range(20):
+            nc.tensor.matmul(out=warm[:, 0:P], lhsT=ident_bf[:], rhs=ident_bf[:], start=True, stop=True)
+        transpose_x(0, "c", 0)
+        transpose_x(0, "c", 1)
         spread = rows.tile([P, CW], F32, tag="rows", name="spread")
         nc.tensor.transpose(spread[:, 0:P], bias_f32[:], ident[:])
         for n, b in enumerate((B_I, B_F)):
@@ -411,7 +416,11 @@ def tile_mlstmblock_pb_t_kernel(
             n_new(cell, nc.gpsimd)
             for nm in ("c", "l"):
                 for half_no in range(2):
-                    prepare_x(ahead, nm, half_no)
+                    if j > -2 or nm == "l":
+                        transpose_x(ahead, nm, half_no)
+                    regroup_x(ahead, nm, half_no)
+                if j == -2 and nm == "c":
+                    nc.scalar.copy(out=w_grouped[:, W_I], in_=w_raw[:, 1].rearrange("p j c -> p c j"))
             sum_of_squares(last)
             leave(gates, "k")
             load_x(j + 6, "c")
@@ -429,7 +438,6 @@ def tile_mlstmblock_pb_t_kernel(
             to_rows(gates, "k")
             quantise_x(ahead, "c")
             if j == -2:
-                nc.scalar.copy(out=w_grouped[:, W_I], in_=w_raw[:, 1].rearrange("p j c -> p c j"))
                 group_weights(W_K, 2)
                 quantise_weights(W_I, W_K + 1)
                 shift_m(0, nc.vector)
@@ -451,6 +459,10 @@ def tile_mlstmblock_pb_t_kernel(
             square_root(last)
             if j >= -1:
                 shift_m(j + 3, nc.gpsimd)
+            if j == -2:
+                warm = rows.tile([P, CW], F32, tag="rows", name="warm")
+                for n in range(8):
+                    nc.tensor.matmul(out=warm[:, 0:P], lhsT=ident_bf[:], rhs=ident_bf[:], start=True, stop=True)
             project_d(ahead)
             project(ahead, "i")
             project(ahead, "k")

@@ -63,9 +63,14 @@ def tile_mlstmblock_pb_t_kernel(
         name="states", bufs=1
     ) as states, tc.tile_pool(name="quant", bufs=2) as quant, tc.tile_pool(name="work", bufs=3) as work, tc.tile_pool(
         name="outs", bufs=3
-    ) as outs, tc.psum_pool(name="front", bufs=4) as front, tc.psum_pool(
-        name="dsum", bufs=1
-    ) as dsum, tc.psum_pool(name="rows", bufs=3) as rows, tc.manual_schedule():
+    ) as outs, tc.psum_pool(
+        name="banks", bufs=1
+    ) as banks, tc.manual_schedule():
+        BANK = {"xc0": 0, "xc1": 1, "xl0": 2, "xl1": 3, "v": 0, "o": 1, "q": 2, "k": 2, "i": 3, "d": 4, "v_rows": 5, "i_rows": 5, "k_rows": 6, "o_rows": 6, "q_rows": 7}
+
+        def bank_tile(step, shape, dtype=F32):
+            return banks.tile(shape, dtype, tag="bank%d" % BANK[step], name="bank%d" % BANK[step])
+
         kept = {}
 
         def absent(c):
@@ -166,7 +171,7 @@ def tile_mlstmblock_pb_t_kernel(
             if absent(c) or 2 * half_no >= SIZES[c]:
                 return
             words = kept[("x" + nm, c)][:].bitcast(F32)
-            bank = front.tile([P, CW], F32, tag="front", name="xT")
+            bank = bank_tile("x%s%d" % (nm, half_no), [P, CW])
             for tt in range(2):
                 t = 2 * half_no + tt
                 for u in range(2):
@@ -218,7 +223,7 @@ def tile_mlstmblock_pb_t_kernel(
             if absent(c):
                 return
             codes, scales = kept[("mxc", c)]
-            acc = dsum.tile([P, SIZES[c] * H], F32, tag="d_sum", name="d_sum")
+            acc = bank_tile("d", [P, SIZES[c] * H])
             for t in range(SIZES[c]):
                 x_tile = codes[:, t * P : (t + 1) * P], scales[:, t * P : (t + 1) * P]
                 out = acc[:, t * H : (t + 1) * H]
@@ -231,7 +236,7 @@ def tile_mlstmblock_pb_t_kernel(
                 return
             g, nm = {"i": (W_I, "c"), "k": (W_K, "c"), "q": (W_Q, "c"), "v": (W_V, "l"), "o": (W_O, "l")}[name]
             codes, scales = kept[("mx" + nm, c)]
-            acc = front.tile([P, SIZES[c] * H], F32, tag="front", name="acc")
+            acc = bank_tile(name, [P, SIZES[c] * H])
             matmul_mx(acc[:], weight(g), (codes[:], scales[:]), True, True)
             kept[("acc_" + name, c)] = acc
 
@@ -253,7 +258,7 @@ def tile_mlstmblock_pb_t_kernel(
             if absent(c):
                 return
             src = kept[(name + "_cols", c)]
-            bank = rows.tile([P, SIZES[c] * H], F32, tag="rows", name=name + "_rows")
+            bank = bank_tile(name + "_rows", [P, SIZES[c] * H])
             for t in range(SIZES[c]):
                 nc.tensor.transpose(bank[:, t * H : (t + 1) * H], src[:, t * P : (t + 1) * P], ident[:])
             kept[(name, c)] = bank
@@ -371,12 +376,12 @@ def tile_mlstmblock_pb_t_kernel(
                 )
             store(c, "h")
 
-        warm = rows.tile([P, CW], F32, tag="rows", name="warm")
+        warm = bank_tile("v_rows", [P, CW])
         for n in range(20):
             nc.tensor.matmul(out=warm[:, 0:P], lhsT=ident_bf[:], rhs=ident_bf[:], start=True, stop=True)
         transpose_x(0, "c", 0)
         transpose_x(0, "c", 1)
-        spread = rows.tile([P, CW], F32, tag="rows", name="spread")
+        spread = bank_tile("q_rows", [P, CW])
         nc.tensor.transpose(spread[:, 0:P], bias_f32[:], ident[:])
         for n, b in enumerate((B_I, B_F)):
             nc.tensor.matmul(
@@ -408,12 +413,16 @@ def tile_mlstmblock_pb_t_kernel(
         for j in range(-2, CHUNKS + 2):
             ahead, gates, cell, last, done = j + 2, j + 1, j, j - 1, j - 2
 
-            ik(cell)
-            fn(cell)
-            nq(last)
+            leave(gates, "k")
             leave(gates, "i")
+            ik(cell)
             to_rows(cell, "v")
+            if j >= -1:
+                shift_m(j + 3, nc.gpsimd)
+            fn(cell)
+            fc(cell)
             n_new(cell, nc.gpsimd)
+            nq(last)
             for nm in ("c", "l"):
                 for half_no in range(2):
                     if j > -2 or nm == "l":
@@ -421,31 +430,37 @@ def tile_mlstmblock_pb_t_kernel(
                     regroup_x(ahead, nm, half_no)
                 if j == -2 and nm == "c":
                     nc.scalar.copy(out=w_grouped[:, W_I], in_=w_raw[:, 1].rearrange("p j c -> p c j"))
-            sum_of_squares(last)
-            leave(gates, "k")
             load_x(j + 6, "c")
             load_x(j + 6, "l")
-            ikv(cell)
-            fc(cell)
-            cq(last)
-            d_new(gates)
-            c_new(cell, nc.gpsimd)
             to_rows(last, "o")
+            ikv(cell)
+            c_new(cell, nc.gpsimd)
+            add_epsilon(done)
+            sum_of_squares(last)
             for name in ("v", "o", "q"):
                 project(gates, name)
                 leave(gates, name)
+            cq(last)
+            d_new(gates)
+            exponential(gates, "ei", -1.0)
+            exponential(gates, "ef", 1.0)
             to_rows(gates, "i")
-            to_rows(gates, "k")
             quantise_x(ahead, "c")
+            ho(last)
             if j == -2:
                 group_weights(W_K, 2)
                 quantise_weights(W_I, W_K + 1)
                 shift_m(0, nc.vector)
                 shift_m(1, nc.gpsimd)
-            add_epsilon(done)
-            ho(last)
+            to_rows(cell, "q")
+            to_rows(gates, "k")
             reciprocal(done)
-            m_new(gates)
+            if j == -2:
+                warm = bank_tile("v_rows", [P, CW])
+                for n in range(8):
+                    nc.tensor.matmul(out=warm[:, 0:P], lhsT=ident_bf[:], rhs=ident_bf[:], start=True, stop=True)
+            project_d(ahead)
+            project(ahead, "k")
             quantise_x(ahead, "l")
             if j == -2:
                 for g_no, raw_no in ((W_Q, 3), (W_V, 4)):
@@ -453,17 +468,7 @@ def tile_mlstmblock_pb_t_kernel(
                 group_weights(W_O, 5)
                 quantise_weights(W_Q, W_Q + 1)
                 quantise_weights(W_V, W_O + 1)
-            scale_rows(done)
-            exponential(gates, "ei", -1.0)
-            exponential(gates, "ef", 1.0)
             square_root(last)
-            if j >= -1:
-                shift_m(j + 3, nc.gpsimd)
-            if j == -2:
-                warm = rows.tile([P, CW], F32, tag="rows", name="warm")
-                for n in range(8):
-                    nc.tensor.matmul(out=warm[:, 0:P], lhsT=ident_bf[:], rhs=ident_bf[:], start=True, stop=True)
-            project_d(ahead)
             project(ahead, "i")
-            project(ahead, "k")
-            to_rows(cell, "q")
+            m_new(gates)
+            scale_rows(done)

@@ -417,8 +417,6 @@ def tile_mlstmblock_pb_t_kernel(
             leave(gates, "i")
             ik(cell)
             to_rows(cell, "v")
-            if j >= -1:
-                shift_m(j + 3, nc.gpsimd)
             fn(cell)
             fc(cell)
             n_new(cell, nc.gpsimd)
@@ -451,7 +449,7 @@ def tile_mlstmblock_pb_t_kernel(
                 group_weights(W_K, 2)
                 quantise_weights(W_I, W_K + 1)
                 shift_m(0, nc.vector)
-                shift_m(1, nc.gpsimd)
+                shift_m(1, nc.vector)
             to_rows(cell, "q")
             to_rows(gates, "k")
             reciprocal(done)
@@ -472,3 +470,5 @@ def tile_mlstmblock_pb_t_kernel(
             project(ahead, "i")
             m_new(gates)
             scale_rows(done)
+            if j >= -1:
+                shift_m(j + 3, nc.vector)

@@ -420,31 +420,39 @@ def tile_mlstmblock_pb_t_kernel(
             fn(cell)
             fc(cell)
             n_new(cell, nc.gpsimd)
-            nq(last)
-            for nm in ("c", "l"):
-                for half_no in range(2):
-                    if j > -2 or nm == "l":
-                        transpose_x(ahead, nm, half_no)
-                    regroup_x(ahead, nm, half_no)
-                if j == -2 and nm == "c":
-                    nc.scalar.copy(out=w_grouped[:, W_I], in_=w_raw[:, 1].rearrange("p j c -> p c j"))
+            if j > -2:
+                transpose_x(ahead, "c", 0)
+            regroup_x(ahead, "c", 0)
+            if j > -2:
+                transpose_x(ahead, "c", 1)
+            regroup_x(ahead, "c", 1)
+            if j == -2:
+                nc.scalar.copy(out=w_grouped[:, W_I], in_=w_raw[:, 1].rearrange("p j c -> p c j"))
+            transpose_x(ahead, "l", 0)
+            regroup_x(ahead, "l", 0)
+            transpose_x(ahead, "l", 1)
+            regroup_x(ahead, "l", 1)
             load_x(j + 6, "c")
             load_x(j + 6, "l")
             to_rows(last, "o")
             ikv(cell)
+            nq(last)
             c_new(cell, nc.gpsimd)
             add_epsilon(done)
+            project(gates, "v")
+            leave(gates, "v")
             sum_of_squares(last)
-            for name in ("v", "o", "q"):
-                project(gates, name)
-                leave(gates, name)
+            project(gates, "o")
+            leave(gates, "o")
+            project(gates, "q")
+            leave(gates, "q")
             cq(last)
             d_new(gates)
             exponential(gates, "ei", -1.0)
             exponential(gates, "ef", 1.0)
             to_rows(gates, "i")
-            quantise_x(ahead, "c")
             ho(last)
+            quantise_x(ahead, "c")
             if j == -2:
                 group_weights(W_K, 2)
                 quantise_weights(W_I, W_K + 1)

@@ -93,7 +93,13 @@ def tile_mlstmblock_pb_t_kernel(
             if absent(c):
                 return
             x_sb = xin.tile([P, SIZES[c] * K], BF16, tag="x" + nm, name="x" + nm)
-            nc.sync.dma_start(out=x_sb[:].rearrange("p (t k) -> p t k", k=K), in_=x_views[nm][:, tiles(c), :])
+            parts = 2 if c == 0 else 1
+            n = SIZES[c] // parts
+            for i in range(parts):
+                nc.sync.dma_start(
+                    out=x_sb[:, i * n * K : (i + 1) * n * K].rearrange("p (t k) -> p t k", k=K),
+                    in_=x_views[nm][:, FIRST[c] + i * n : FIRST[c] + (i + 1) * n, :],
+                )
             kept[("x" + nm, c)] = x_sb
 
         m_all = const.tile([P, TILES * H], BF16)
@@ -258,7 +264,7 @@ def tile_mlstmblock_pb_t_kernel(
             if absent(c):
                 return
             src = kept[(name + "_cols", c)]
-            bank = bank_tile(name + "_rows", [P, SIZES[c] * H])
+            bank = bank_tile("xl0" if c == CHUNKS - 1 and name == "q" else name + "_rows", [P, SIZES[c] * H])
             for t in range(SIZES[c]):
                 nc.tensor.transpose(bank[:, t * H : (t + 1) * H], src[:, t * P : (t + 1) * P], ident[:])
             kept[(name, c)] = bank
@@ -336,7 +342,7 @@ def tile_mlstmblock_pb_t_kernel(
         def sum_of_squares(c):
             if absent(c):
                 return
-            squares = work.tile([P, SIZES[c] * H], F32, tag="squares", name="squares")
+            squares = const.tile([P, SIZES[c] * H], F32, tag="squares", name="squares")
             ss = small(c, "ss")
             for t in range(SIZES[c]):
                 nc.scalar.activation(
@@ -377,7 +383,7 @@ def tile_mlstmblock_pb_t_kernel(
             store(c, "h")
 
         warm = bank_tile("v_rows", [P, CW])
-        for n in range(20):
+        for n in range(18):
             nc.tensor.matmul(out=warm[:, 0:P], lhsT=ident_bf[:], rhs=ident_bf[:], start=True, stop=True)
         transpose_x(0, "c", 0)
         transpose_x(0, "c", 1)
@@ -410,7 +416,7 @@ def tile_mlstmblock_pb_t_kernel(
         nc.vector.tensor_scalar_mul(out=w_grouped[:, W_NI], in0=w_raw[:, 1].rearrange("p j c -> p c j"), scalar1=-1.0)
         quantise_weights(W_F, W_NI + 1)
 
-        for j in range(-2, CHUNKS + 2):
+        for j in range(-2, CHUNKS + 1):
             ahead, gates, cell, last, done = j + 2, j + 1, j, j - 1, j - 2
 
             leave(gates, "k")
@@ -436,12 +442,14 @@ def tile_mlstmblock_pb_t_kernel(
             load_x(j + 6, "l")
             to_rows(last, "o")
             ikv(cell)
-            nq(last)
+            if last < CHUNKS - 1:
+                nq(last)
             c_new(cell, nc.gpsimd)
             add_epsilon(done)
             project(gates, "v")
             leave(gates, "v")
-            sum_of_squares(last)
+            if last < CHUNKS - 1:
+                sum_of_squares(last)
             project(gates, "o")
             leave(gates, "o")
             project(gates, "q")
@@ -460,6 +468,9 @@ def tile_mlstmblock_pb_t_kernel(
                 shift_m(1, nc.vector)
             to_rows(cell, "q")
             to_rows(gates, "k")
+            if cell == CHUNKS - 1:
+                nq(cell)
+                sum_of_squares(cell)
             reciprocal(done)
             if j == -2:
                 warm = bank_tile("v_rows", [P, CW])
@@ -474,9 +485,16 @@ def tile_mlstmblock_pb_t_kernel(
                 group_weights(W_O, 5)
                 quantise_weights(W_Q, W_Q + 1)
                 quantise_weights(W_V, W_O + 1)
-            square_root(last)
+            if last < CHUNKS - 1:
+                square_root(last)
+            if cell == CHUNKS - 1:
+                square_root(cell)
             project(ahead, "i")
             m_new(gates)
             scale_rows(done)
+            if last == CHUNKS - 1:
+                add_epsilon(last)
+                reciprocal(last)
+                scale_rows(last)
             if j >= -1:
                 shift_m(j + 3, nc.vector)

@@ -16,13 +16,23 @@ ROWS = 4096
 K = 512
 H = 128
 TILES = ROWS // P
-SIZES = (4, 4, 4, 4, 4, 4, 4, 4)
-CHUNKS = len(SIZES)
-FIRST = tuple(sum(SIZES[:c]) for c in range(CHUNKS))
-CW = 4 * H
+TPC = 4
+CHUNKS = TILES // TPC
+CW = TPC * H
 B_I, B_F, B_K, B_Q, B_V, B_O = range(6)
 W_F, W_NI, W_I, W_K, W_Q, W_V, W_O = range(7)
 FLOPS = 2 * ROWS * K * H * 6
+
+BANK = {
+    "xc0": 0, "v": 0,
+    "xc1": 1, "o": 1,
+    "xl0": 2, "q": 2, "k": 2,
+    "xl1": 3, "i": 3,
+    "d": 4,
+    "v_rows": 5, "i_rows": 5,
+    "k_rows": 6, "o_rows": 6,
+    "q_rows": 7,
+}
 
 
 def tile_mlstmblock_pb_t_kernel(
@@ -63,63 +73,56 @@ def tile_mlstmblock_pb_t_kernel(
         name="states", bufs=1
     ) as states, tc.tile_pool(name="quant", bufs=2) as quant, tc.tile_pool(name="work", bufs=3) as work, tc.tile_pool(
         name="outs", bufs=3
-    ) as outs, tc.psum_pool(
-        name="banks", bufs=1
-    ) as banks, tc.manual_schedule():
-        BANK = {"xc0": 0, "xc1": 1, "xl0": 2, "xl1": 3, "v": 0, "o": 1, "q": 2, "k": 2, "i": 3, "d": 4, "v_rows": 5, "i_rows": 5, "k_rows": 6, "o_rows": 6, "q_rows": 7}
-
-        def bank_tile(step, shape, dtype=F32):
-            return banks.tile(shape, dtype, tag="bank%d" % BANK[step], name="bank%d" % BANK[step])
-
+    ) as outs, tc.psum_pool(name="banks", bufs=1) as banks, tc.manual_schedule():
         kept = {}
 
         def absent(c):
             return c < 0 or c >= CHUNKS
 
+        def bank_tile(step):
+            name = "bank%d" % BANK[step]
+            return banks.tile([P, CW], F32, tag=name, name=name)
+
+        def new(pool, name, c):
+            kept[(name, c)] = pool.tile([P, CW], F32, tag=name, name=name)
+            return kept[(name, c)]
+
+        def new_column(name, c):
+            kept[(name, c)] = work.tile([P, TPC], F32, tag=name, name=name)
+            return kept[(name, c)]
+
         def by_tile(ap):
             return ap.rearrange("p (t h) -> p t h", h=H)
 
-        def new(pool, name, c):
-            kept[(name, c)] = pool.tile([P, SIZES[c] * H], F32, tag=name, name=name)
-            return kept[(name, c)]
-
-        def tiles(c):
-            return slice(FIRST[c], FIRST[c] + SIZES[c])
-
-        def cols(c):
-            return slice(FIRST[c] * H, (FIRST[c] + SIZES[c]) * H)
+        def part(t):
+            return slice(t * H, (t + 1) * H)
 
         def load_x(c, nm):
             if absent(c):
                 return
-            x_sb = xin.tile([P, SIZES[c] * K], BF16, tag="x" + nm, name="x" + nm)
-            parts = 2 if c == 0 else 1
-            n = SIZES[c] // parts
-            for i in range(parts):
+            x_sb = xin.tile([P, TPC * K], BF16, tag="x" + nm, name="x" + nm)
+            step = TPC // 2 if c == 0 else TPC
+            for t in range(0, TPC, step):
                 nc.sync.dma_start(
-                    out=x_sb[:, i * n * K : (i + 1) * n * K].rearrange("p (t k) -> p t k", k=K),
-                    in_=x_views[nm][:, FIRST[c] + i * n : FIRST[c] + (i + 1) * n, :],
+                    out=x_sb[:, t * K : (t + step) * K].rearrange("p (t k) -> p t k", k=K),
+                    in_=x_views[nm][:, c * TPC + t : c * TPC + t + step, :],
                 )
             kept[("x" + nm, c)] = x_sb
 
         m_all = const.tile([P, TILES * H], BF16)
 
-        def load_state(c, count):
-            w = sum(SIZES[c : c + count]) * H
-            for nm, view in (("n", n_view), ("c", c_view)):
-                st = states.tile([P, w], BF16, tag="%s%d" % (nm, c), name="%s%d" % (nm, c))
-                nc.sync.dma_start(out=by_tile(st[:]), in_=view[:, FIRST[c] : FIRST[c] + w // H, :])
-                for i in range(c, c + count):
-                    kept[(nm + "_prev", i)] = st[:, (FIRST[i] - FIRST[c]) * H : (FIRST[i] - FIRST[c] + SIZES[i]) * H]
-
         def load_m(t0, t1):
             nc.sync.dma_start(out=by_tile(m_all[:, t0 * H : t1 * H]), in_=m_view[:, t0:t1, :])
 
+        def load_state(c):
+            for nm, view in (("n", n_view), ("c", c_view)):
+                st = states.tile([P, CW], BF16, tag="%s%d" % (nm, c), name="%s%d" % (nm, c))
+                nc.sync.dma_start(out=by_tile(st[:]), in_=view[:, c * TPC : (c + 1) * TPC, :])
+                kept[(nm + "_prev", c)] = st
+
         def store(c, nm):
-            if absent(c):
-                return
             nc.sync.dma_start(
-                out=out_views[nm][:, tiles(c), :], in_=by_tile(kept[(nm + "_t", c)][:])
+                out=out_views[nm][:, c * TPC : (c + 1) * TPC, :], in_=by_tile(kept[(nm + "_t", c)][:])
             )
 
         load_x(0, "c")
@@ -132,25 +135,25 @@ def tile_mlstmblock_pb_t_kernel(
             nc.sync.dma_start(out=w_raw[:, g, :, :], in_=w_ap.rearrange("(q j) c -> q j c", j=4))
             if g == 1:
                 load_x(0, "l")
-                load_m(0, 4)
+                load_m(0, TPC)
         load_x(1, "c")
         load_x(1, "l")
-        load_m(4, 8)
-        load_state(0, 1)
+        load_m(TPC, 2 * TPC)
+        load_state(0)
         load_x(2, "c")
         load_x(2, "l")
-        load_m(8, TILES)
-        load_state(1, 1)
+        load_m(2 * TPC, TILES)
+        load_state(1)
         load_x(3, "c")
         load_x(3, "l")
         for c in range(2, CHUNKS):
-            load_state(c, 1)
+            load_state(c)
 
         zero = const.tile([P, 1], F32)
         nc.vector.memset(zero[:], 0.0)
         one = const.tile([P, 1], F32)
         nc.scalar.activation(out=one[:], in_=zero[:], func=ACT.Exp)
-        half = const.tile([P, 4], F32)
+        half = const.tile([P, TPC], F32)
         nc.vector.memset(half[:], 0.5)
         ident = const.tile([P, P], F32)
         make_identity(nc, ident[:])
@@ -163,8 +166,8 @@ def tile_mlstmblock_pb_t_kernel(
         w_codes = const.tile([P, 7 * H], U32, align_bytes=64)
         w_scales = const.tile([P, 7 * H], U8, align_bytes=64)
 
-        def group_weights(out_g, raw_g):
-            nc.vector.tensor_copy(out=w_grouped[:, out_g], in_=w_raw[:, raw_g].rearrange("p j c -> p c j"))
+        def group_weights(copy, out_g, raw_g):
+            copy(out=w_grouped[:, out_g], in_=w_raw[:, raw_g].rearrange("p j c -> p c j"))
 
         def quantise_weights(g0, g1):
             nc.vector.quantize_mx(
@@ -174,26 +177,26 @@ def tile_mlstmblock_pb_t_kernel(
             )
 
         def transpose_x(c, nm, half_no):
-            if absent(c) or 2 * half_no >= SIZES[c]:
+            if absent(c):
                 return
             words = kept[("x" + nm, c)][:].bitcast(F32)
-            bank = bank_tile("x%s%d" % (nm, half_no), [P, CW])
+            bank = bank_tile("x%s%d" % (nm, half_no))
             for tt in range(2):
                 t = 2 * half_no + tt
                 for u in range(2):
                     nc.tensor.transpose(
-                        bank[:, u * 256 + tt * P : u * 256 + (tt + 1) * P],
-                        words[:, t * 256 + u : (t + 1) * 256 : 2],
+                        bank[:, u * 2 * P + tt * P : u * 2 * P + (tt + 1) * P],
+                        words[:, t * (K // 2) + u : (t + 1) * (K // 2) : 2],
                         ident[:],
                     )
             kept[("xT" + nm, c, half_no)] = bank
 
         def regroup_x(c, nm, half_no):
-            if absent(c) or 2 * half_no >= SIZES[c]:
+            if absent(c):
                 return
             if half_no == 0:
                 kept[("grouped" + nm, c)] = quant.tile(
-                    [P, SIZES[c] * K], BF16, tag="grouped" + nm, name="grouped" + nm, align_bytes=64
+                    [P, TPC * K], BF16, tag="grouped" + nm, name="grouped" + nm, align_bytes=64
                 )
             words = kept[("grouped" + nm, c)][:].bitcast(F32)
             nc.scalar.copy(
@@ -204,11 +207,9 @@ def tile_mlstmblock_pb_t_kernel(
         def quantise_x(c, nm):
             if absent(c):
                 return
-            codes = quant.tile([P, SIZES[c] * H], U32, tag="codes" + nm, name="codes" + nm, align_bytes=64)
-            scales = quant.tile([P, SIZES[c] * H], U8, tag="scales" + nm, name="scales" + nm, align_bytes=64)
-            nc.vector.quantize_mx(
-                out=codes[:].bitcast(FP8X4), scales=scales[:], in_=kept[("grouped" + nm, c)][:]
-            )
+            codes = quant.tile([P, CW], U32, tag="codes" + nm, name="codes" + nm, align_bytes=64)
+            scales = quant.tile([P, CW], U8, tag="scales" + nm, name="scales" + nm, align_bytes=64)
+            nc.vector.quantize_mx(out=codes[:].bitcast(FP8X4), scales=scales[:], in_=kept[("grouped" + nm, c)][:])
             kept[("mx" + nm, c)] = (codes, scales)
 
         def matmul_mx(out, lhs, rhs, first, last):
@@ -229,22 +230,21 @@ def tile_mlstmblock_pb_t_kernel(
             if absent(c):
                 return
             codes, scales = kept[("mxc", c)]
-            acc = bank_tile("d", [P, SIZES[c] * H])
-            for t in range(SIZES[c]):
-                x_tile = codes[:, t * P : (t + 1) * P], scales[:, t * P : (t + 1) * P]
-                out = acc[:, t * H : (t + 1) * H]
-                matmul_mx(out, x_tile, weight(W_F), True, False)
-                matmul_mx(out, x_tile, weight(W_NI), False, True)
-            kept[("d_sum", c)] = acc
+            bank = bank_tile("d")
+            for t in range(TPC):
+                x_tile = codes[:, part(t)], scales[:, part(t)]
+                matmul_mx(bank[:, part(t)], x_tile, weight(W_F), True, False)
+                matmul_mx(bank[:, part(t)], x_tile, weight(W_NI), False, True)
+            kept[("d_sum", c)] = bank
 
         def project(c, name):
             if absent(c):
                 return
             g, nm = {"i": (W_I, "c"), "k": (W_K, "c"), "q": (W_Q, "c"), "v": (W_V, "l"), "o": (W_O, "l")}[name]
             codes, scales = kept[("mx" + nm, c)]
-            acc = bank_tile(name, [P, SIZES[c] * H])
-            matmul_mx(acc[:], weight(g), (codes[:], scales[:]), True, True)
-            kept[("acc_" + name, c)] = acc
+            bank = bank_tile(name)
+            matmul_mx(bank[:], weight(g), (codes[:], scales[:]), True, True)
+            kept[(name + "_sum", c)] = bank
 
         def leave(c, name):
             if absent(c):
@@ -257,30 +257,31 @@ def tile_mlstmblock_pb_t_kernel(
                 "o": (ACT.Tanh, bo_half[:], 0.5),
             }[name]
             nc.scalar.activation(
-                out=new(work, name + "_cols", c)[:], in_=kept[("acc_" + name, c)][:], func=func, bias=bias, scale=scale
+                out=new(work, name + "_cols", c)[:], in_=kept[(name + "_sum", c)][:], func=func, bias=bias, scale=scale
             )
 
         def to_rows(c, name):
             if absent(c):
                 return
-            src = kept[(name + "_cols", c)]
-            bank = bank_tile("xl0" if c == CHUNKS - 1 and name == "q" else name + "_rows", [P, SIZES[c] * H])
-            for t in range(SIZES[c]):
-                nc.tensor.transpose(bank[:, t * H : (t + 1) * H], src[:, t * P : (t + 1) * P], ident[:])
+            cols = kept[(name + "_cols", c)]
+            bank = bank_tile("xl0" if name == "q" and c == CHUNKS - 1 else name + "_rows")
+            for t in range(TPC):
+                nc.tensor.transpose(bank[:, part(t)], cols[:, part(t)], ident[:])
             kept[(name, c)] = bank
 
         m_shifted = const.tile([P, TILES * H], F32)
 
-        def shift_m(c, engine):
+        def shift_m(c):
             if absent(c):
                 return
-            engine.tensor_tensor(
-                out=by_tile(m_shifted[:, cols(c)]),
-                in0=by_tile(m_all[:, cols(c)]),
-                in1=bf_minus_bi[:].unsqueeze(1).to_broadcast([P, SIZES[c], H]),
+            columns = slice(c * CW, (c + 1) * CW)
+            nc.vector.tensor_tensor(
+                out=by_tile(m_shifted[:, columns]),
+                in0=by_tile(m_all[:, columns]),
+                in1=bf_minus_bi[:].unsqueeze(1).to_broadcast([P, TPC, H]),
                 op=ALU.add,
             )
-            kept[("m_shifted", c)] = m_shifted[:, cols(c)]
+            kept[("m_shifted", c)] = m_shifted[:, columns]
 
         def two(engine, pool, out_name, c, a, b, op):
             if absent(c):
@@ -297,97 +298,84 @@ def tile_mlstmblock_pb_t_kernel(
         def d_new(c):
             two(nc.vector, work, "d", c, "d_sum", "m_shifted", ALU.add)
 
-        def m_new(c):
-            three(outs, "m_t", c, "d", 0.0, ALU.max, "i", ALU.add)
-            store(c, "m")
-
-        def ik(c):
-            three(work, "ik", c, "ei", 1.0, ALU.min, "k", ALU.mult)
-
-        def fn(c):
-            three(work, "fn", c, "ef", 1.0, ALU.min, "n_prev", ALU.mult)
-
-        def fc(c):
-            three(work, "fc", c, "ef", 1.0, ALU.min, "c_prev", ALU.mult)
-
-        def ikv(c):
-            two(nc.vector, work, "ikv", c, "v", "ik", ALU.mult)
-
-        def n_new(c, engine):
-            two(engine, outs, "n_t", c, "fn", "ik", ALU.add)
-            store(c, "n")
-
-        def c_new(c, engine):
-            two(engine, outs, "c_t", c, "fc", "ikv", ALU.add)
-            store(c, "c")
-
-        def nq(c):
-            two(nc.vector, work, "nq", c, "q", "n_t", ALU.mult)
-
-        def cq(c):
-            two(nc.vector, work, "cq", c, "q", "c_t", ALU.mult)
-
-        def ho(c):
-            three(work, "ho", c, "o", 1.0, ALU.add, "cq", ALU.mult)
-
         def exponential(c, out_name, sign):
             if absent(c):
                 return
             nc.scalar.activation(out=new(work, out_name, c)[:], in_=kept[("d", c)][:], func=ACT.Exp, scale=sign)
 
-        def small(c, name):
-            kept[(name, c)] = work.tile([P, SIZES[c]], F32, tag=name, name=name)
-            return kept[(name, c)]
+        def m_new(c):
+            three(outs, "m_t", c, "d", 0.0, ALU.max, "i", ALU.add)
+            if not absent(c):
+                store(c, "m")
+
+        def ik(c):
+            three(work, "ik", c, "exp_minus_d", 1.0, ALU.min, "k", ALU.mult)
+
+        def forget(c, state):
+            three(work, "f" + state, c, "exp_d", 1.0, ALU.min, state + "_prev", ALU.mult)
+
+        def ikv(c):
+            two(nc.vector, work, "ikv", c, "v", "ik", ALU.mult)
+
+        def state_new(c, state, update):
+            two(nc.gpsimd, outs, state + "_t", c, "f" + state, update, ALU.add)
+            if not absent(c):
+                store(c, state)
+
+        def times_q(c, state):
+            two(nc.vector, work, state + "q", c, "q", state + "_t", ALU.mult)
+
+        def open_gate(c):
+            three(work, "ocq", c, "o", 1.0, ALU.add, "cq", ALU.mult)
 
         def sum_of_squares(c):
             if absent(c):
                 return
-            squares = const.tile([P, SIZES[c] * H], F32, tag="squares", name="squares")
-            ss = small(c, "ss")
-            for t in range(SIZES[c]):
+            squares = const.tile([P, CW], F32, tag="squares", name="squares")
+            total = new_column("total", c)
+            for t in range(TPC):
                 nc.scalar.activation(
-                    out=squares[:, t * H : (t + 1) * H],
-                    in_=kept[("nq", c)][:, t * H : (t + 1) * H],
+                    out=squares[:, part(t)],
+                    in_=kept[("nq", c)][:, part(t)],
                     func=ACT.Square,
                     scale=2.0,
-                    accum_out=ss[:, t : t + 1],
+                    accum_out=total[:, t : t + 1],
                 )
 
         def square_root(c):
             if absent(c):
                 return
-            nc.gpsimd.tensor_tensor(
-                out=small(c, "root")[:], in0=kept[("ss", c)][:], in1=half[:, 0 : SIZES[c]], op=ALU.pow
-            )
+            nc.gpsimd.tensor_tensor(out=new_column("norm", c)[:], in0=kept[("total", c)][:], in1=half[:], op=ALU.pow)
 
         def add_epsilon(c):
             if absent(c):
                 return
-            nc.vector.tensor_scalar_add(out=small(c, "denom2")[:], in0=kept[("root", c)][:], scalar1=2.0e-6)
+            nc.vector.tensor_scalar_add(out=new_column("denom", c)[:], in0=kept[("norm", c)][:], scalar1=2.0e-6)
 
         def reciprocal(c):
             if absent(c):
                 return
-            nc.vector.reciprocal(out=small(c, "scale")[:], in_=kept[("denom2", c)][:])
+            nc.vector.reciprocal(out=new_column("scale", c)[:], in_=kept[("denom", c)][:])
 
         def scale_rows(c):
             if absent(c):
                 return
             h_t = new(outs, "h_t", c)
-            for t in range(SIZES[c]):
+            for t in range(TPC):
                 nc.vector.tensor_scalar_mul(
-                    out=h_t[:, t * H : (t + 1) * H],
-                    in0=kept[("ho", c)][:, t * H : (t + 1) * H],
-                    scalar1=kept[("scale", c)][:, t : t + 1],
+                    out=h_t[:, part(t)], in0=kept[("ocq", c)][:, part(t)], scalar1=kept[("scale", c)][:, t : t + 1]
                 )
             store(c, "h")
 
-        warm = bank_tile("v_rows", [P, CW])
-        for n in range(18):
-            nc.tensor.matmul(out=warm[:, 0:P], lhsT=ident_bf[:], rhs=ident_bf[:], start=True, stop=True)
+        def keep_clock(count):
+            bank = bank_tile("v_rows")
+            for n in range(count):
+                nc.tensor.matmul(out=bank[:, 0:P], lhsT=ident_bf[:], rhs=ident_bf[:], start=True, stop=True)
+
+        keep_clock(18)
         transpose_x(0, "c", 0)
         transpose_x(0, "c", 1)
-        spread = bank_tile("q_rows", [P, CW])
+        spread = bank_tile("q_rows")
         nc.tensor.transpose(spread[:, 0:P], bias_f32[:], ident[:])
         for n, b in enumerate((B_I, B_F)):
             nc.tensor.matmul(
@@ -407,45 +395,40 @@ def tile_mlstmblock_pb_t_kernel(
         nc.vector.tensor_scalar_mul(out=bk_scaled[:], in0=bias_col[:, B_K : B_K + 1], scalar1=k_scale)
         bf_minus_bi = const.tile([P, H], F32)
         nc.vector.tensor_tensor(out=bf_minus_bi[:], in0=spread[:, 2 * P : 3 * P], in1=bi_row[:], op=ALU.subtract)
-
-        def prepare_x(c, nm, half_no):
-            transpose_x(c, nm, half_no)
-            regroup_x(c, nm, half_no)
-
-        group_weights(W_F, 0)
+        group_weights(nc.vector.tensor_copy, W_F, 0)
         nc.vector.tensor_scalar_mul(out=w_grouped[:, W_NI], in0=w_raw[:, 1].rearrange("p j c -> p c j"), scalar1=-1.0)
         quantise_weights(W_F, W_NI + 1)
 
         for j in range(-2, CHUNKS + 1):
             ahead, gates, cell, last, done = j + 2, j + 1, j, j - 1, j - 2
+            head = j == -2
+            tail = j == CHUNKS - 1
 
             leave(gates, "k")
             leave(gates, "i")
             ik(cell)
             to_rows(cell, "v")
-            fn(cell)
-            fc(cell)
-            n_new(cell, nc.gpsimd)
-            if j > -2:
-                transpose_x(ahead, "c", 0)
-            regroup_x(ahead, "c", 0)
-            if j > -2:
-                transpose_x(ahead, "c", 1)
-            regroup_x(ahead, "c", 1)
-            if j == -2:
-                nc.scalar.copy(out=w_grouped[:, W_I], in_=w_raw[:, 1].rearrange("p j c -> p c j"))
-            transpose_x(ahead, "l", 0)
-            regroup_x(ahead, "l", 0)
-            transpose_x(ahead, "l", 1)
-            regroup_x(ahead, "l", 1)
+            forget(cell, "n")
+            forget(cell, "c")
+            state_new(cell, "n", "ik")
+
+            for nm in ("c", "l"):
+                for half_no in range(2):
+                    if not (head and nm == "c"):
+                        transpose_x(ahead, nm, half_no)
+                    regroup_x(ahead, nm, half_no)
+                if head and nm == "c":
+                    group_weights(nc.scalar.copy, W_I, 1)
             load_x(j + 6, "c")
             load_x(j + 6, "l")
+
             to_rows(last, "o")
             ikv(cell)
             if last < CHUNKS - 1:
-                nq(last)
-            c_new(cell, nc.gpsimd)
+                times_q(last, "n")
+            state_new(cell, "c", "ikv")
             add_epsilon(done)
+
             project(gates, "v")
             leave(gates, "v")
             if last < CHUNKS - 1:
@@ -454,40 +437,39 @@ def tile_mlstmblock_pb_t_kernel(
             leave(gates, "o")
             project(gates, "q")
             leave(gates, "q")
-            cq(last)
+
+            times_q(last, "c")
             d_new(gates)
-            exponential(gates, "ei", -1.0)
-            exponential(gates, "ef", 1.0)
+            exponential(gates, "exp_minus_d", -1.0)
+            exponential(gates, "exp_d", 1.0)
             to_rows(gates, "i")
-            ho(last)
+            open_gate(last)
             quantise_x(ahead, "c")
-            if j == -2:
-                group_weights(W_K, 2)
+            if head:
+                group_weights(nc.vector.tensor_copy, W_K, 2)
                 quantise_weights(W_I, W_K + 1)
-                shift_m(0, nc.vector)
-                shift_m(1, nc.vector)
+                shift_m(0)
             to_rows(cell, "q")
             to_rows(gates, "k")
-            if cell == CHUNKS - 1:
-                nq(cell)
+            if tail:
+                times_q(cell, "n")
                 sum_of_squares(cell)
             reciprocal(done)
-            if j == -2:
-                warm = bank_tile("v_rows", [P, CW])
-                for n in range(8):
-                    nc.tensor.matmul(out=warm[:, 0:P], lhsT=ident_bf[:], rhs=ident_bf[:], start=True, stop=True)
+
+            if head:
+                keep_clock(8)
             project_d(ahead)
             project(ahead, "k")
             quantise_x(ahead, "l")
-            if j == -2:
-                for g_no, raw_no in ((W_Q, 3), (W_V, 4)):
-                    nc.scalar.copy(out=w_grouped[:, g_no], in_=w_raw[:, raw_no].rearrange("p j c -> p c j"))
-                group_weights(W_O, 5)
+            if head:
+                group_weights(nc.scalar.copy, W_Q, 3)
+                group_weights(nc.scalar.copy, W_V, 4)
+                group_weights(nc.vector.tensor_copy, W_O, 5)
                 quantise_weights(W_Q, W_Q + 1)
                 quantise_weights(W_V, W_O + 1)
             if last < CHUNKS - 1:
                 square_root(last)
-            if cell == CHUNKS - 1:
+            if tail:
                 square_root(cell)
             project(ahead, "i")
             m_new(gates)
@@ -496,5 +478,4 @@ def tile_mlstmblock_pb_t_kernel(
                 add_epsilon(last)
                 reciprocal(last)
                 scale_rows(last)
-            if j >= -1:
-                shift_m(j + 3, nc.vector)
+            shift_m(j + 3)

import math

import concourse.mybir as mybir
from concourse.masks import make_identity

FP8X4 = mybir.dt.float8_e4m3fn_x4
BF16 = mybir.dt.bfloat16
F32 = mybir.dt.float32
U32 = mybir.dt.uint32
U8 = mybir.dt.uint8
ALU = mybir.AluOpType
ACT = mybir.ActivationFunctionType

P = 128
ROWS = 4096
K = 512
H = 128
TILES = ROWS // P
TPC = 4
CHUNKS = TILES // TPC
CW = TPC * H
B_I, B_F, B_K, B_Q, B_V, B_O = range(6)
W_F, W_NI, W_I, W_K, W_Q, W_V, W_O = range(7)
FLOPS = 2 * ROWS * K * H * 6

BANK = {
    "xc0": 0, "v": 0,
    "xc1": 1, "o": 1,
    "xl0": 2, "q": 2, "k": 2,
    "xl1": 3, "i": 3,
    "d": 4,
    "v_rows": 5, "i_rows": 5,
    "k_rows": 6, "o_rows": 6,
    "q_rows": 7,
}


def tile_mlstmblock_pb_t_kernel(
    tc,
    x_conv,
    x_left,
    c_prev,
    n_prev,
    m_prev,
    wq_w,
    wq_b,
    wk_w,
    wk_b,
    wv_w,
    wv_b,
    wi_w,
    wi_b,
    wf_w,
    wf_b,
    wo_w,
    wo_b,
    out_0,
    out_1,
    out_2,
    out_3,
):
    nc = tc.nc
    k_scale = 1.0 / math.sqrt(float(H))

    def by_partition(dram):
        return dram.rearrange("(p t) w -> p t w", t=TILES)

    x_views = {"c": by_partition(x_conv), "l": by_partition(x_left)}
    m_view, n_view, c_view = by_partition(m_prev), by_partition(n_prev), by_partition(c_prev)
    out_views = {"h": by_partition(out_0), "c": by_partition(out_1), "n": by_partition(out_2), "m": by_partition(out_3)}

    with tc.tile_pool(name="const", bufs=1) as const, tc.tile_pool(name="xin", bufs=4) as xin, tc.tile_pool(
        name="states", bufs=1
    ) as states, tc.tile_pool(name="quant", bufs=2) as quant, tc.tile_pool(name="work", bufs=3) as work, tc.tile_pool(
        name="outs", bufs=3
    ) as outs, tc.psum_pool(name="banks", bufs=1) as banks, tc.manual_schedule():
        kept = {}

        def absent(c):
            return c < 0 or c >= CHUNKS

        def bank_tile(step):
            name = "bank%d" % BANK[step]
            return banks.tile([P, CW], F32, tag=name, name=name)

        def new(pool, name, c):
            kept[(name, c)] = pool.tile([P, CW], F32, tag=name, name=name)
            return kept[(name, c)]

        def new_column(name, c):
            kept[(name, c)] = work.tile([P, TPC], F32, tag=name, name=name)
            return kept[(name, c)]

        def by_tile(ap):
            return ap.rearrange("p (t h) -> p t h", h=H)

        def part(t):
            return slice(t * H, (t + 1) * H)

        def load_x(c, nm):
            if absent(c):
                return
            x_sb = xin.tile([P, TPC * K], BF16, tag="x" + nm, name="x" + nm)
            step = TPC // 2 if c == 0 else TPC
            for t in range(0, TPC, step):
                nc.sync.dma_start(
                    out=x_sb[:, t * K : (t + step) * K].rearrange("p (t k) -> p t k", k=K),
                    in_=x_views[nm][:, c * TPC + t : c * TPC + t + step, :],
                )
            kept[("x" + nm, c)] = x_sb

        m_all = const.tile([P, TILES * H], BF16)

        def load_m(t0, t1):
            nc.sync.dma_start(out=by_tile(m_all[:, t0 * H : t1 * H]), in_=m_view[:, t0:t1, :])

        def load_state(c):
            for nm, view in (("n", n_view), ("c", c_view)):
                st = states.tile([P, CW], BF16, tag="%s%d" % (nm, c), name="%s%d" % (nm, c))
                nc.sync.dma_start(out=by_tile(st[:]), in_=view[:, c * TPC : (c + 1) * TPC, :])
                kept[(nm + "_prev", c)] = st

        def store(c, nm):
            nc.sync.dma_start(
                out=out_views[nm][:, c * TPC : (c + 1) * TPC, :], in_=by_tile(kept[(nm + "_t", c)][:])
            )

        load_x(0, "c")
        bias_rows = const.tile([P, P], BF16)
        nc.vector.memset(bias_rows[:], 0.0)
        for b, b_ap in ((B_I, wi_b), (B_F, wf_b), (B_K, wk_b), (B_Q, wq_b), (B_V, wv_b), (B_O, wo_b)):
            nc.sync.dma_start(out=bias_rows[b : b + 1, :], in_=b_ap.unsqueeze(0))
        w_raw = const.tile([P, 6, 4, H], BF16)
        for g, w_ap in enumerate((wf_w, wi_w, wk_w[0], wq_w[0], wv_w[0], wo_w)):
            nc.sync.dma_start(out=w_raw[:, g, :, :], in_=w_ap.rearrange("(q j) c -> q j c", j=4))
            if g == 1:
                load_x(0, "l")
                load_m(0, TPC)
        load_x(1, "c")
        load_x(1, "l")
        load_m(TPC, 2 * TPC)
        load_state(0)
        load_x(2, "c")
        load_x(2, "l")
        load_m(2 * TPC, TILES)
        load_state(1)
        load_x(3, "c")
        load_x(3, "l")
        for c in range(2, CHUNKS):
            load_state(c)

        zero = const.tile([P, 1], F32)
        nc.vector.memset(zero[:], 0.0)
        one = const.tile([P, 1], F32)
        nc.scalar.activation(out=one[:], in_=zero[:], func=ACT.Exp)
        half = const.tile([P, TPC], F32)
        nc.vector.memset(half[:], 0.5)
        ident = const.tile([P, P], F32)
        make_identity(nc, ident[:])
        ident_bf = const.tile([P, P], BF16)
        nc.vector.tensor_copy(out=ident_bf[:], in_=ident[:])
        bias_f32 = const.tile([P, P], F32)
        nc.vector.tensor_copy(out=bias_f32[:], in_=bias_rows[:])

        w_grouped = const.tile([P, 7, H, 4], BF16, align_bytes=64)
        w_codes = const.tile([P, 7 * H], U32, align_bytes=64)
        w_scales = const.tile([P, 7 * H], U8, align_bytes=64)

        def group_weights(copy, out_g, raw_g):
            copy(out=w_grouped[:, out_g], in_=w_raw[:, raw_g].rearrange("p j c -> p c j"))

        def quantise_weights(g0, g1):
            nc.vector.quantize_mx(
                out=w_codes[:, g0 * H : g1 * H].bitcast(FP8X4),
                scales=w_scales[:, g0 * H : g1 * H],
                in_=w_grouped[:, g0:g1].rearrange("p g c t -> p (g c t)"),
            )

        def transpose_x(c, nm, half_no):
            if absent(c):
                return
            words = kept[("x" + nm, c)][:].bitcast(F32)
            bank = bank_tile("x%s%d" % (nm, half_no))
            for tt in range(2):
                t = 2 * half_no + tt
                for u in range(2):
                    nc.tensor.transpose(
                        bank[:, u * 2 * P + tt * P : u * 2 * P + (tt + 1) * P],
                        words[:, t * (K // 2) + u : (t + 1) * (K // 2) : 2],
                        ident[:],
                    )
            kept[("xT" + nm, c, half_no)] = bank

        def regroup_x(c, nm, half_no):
            if absent(c):
                return
            if half_no == 0:
                kept[("grouped" + nm, c)] = quant.tile(
                    [P, TPC * K], BF16, tag="grouped" + nm, name="grouped" + nm, align_bytes=64
                )
            words = kept[("grouped" + nm, c)][:].bitcast(F32)
            nc.scalar.copy(
                out=words[:, half_no * CW : (half_no + 1) * CW].rearrange("p (b u) -> p b u", u=2),
                in_=kept[("xT" + nm, c, half_no)][:].rearrange("p (u b) -> p b u", u=2),
            )

        def quantise_x(c, nm):
            if absent(c):
                return
            codes = quant.tile([P, CW], U32, tag="codes" + nm, name="codes" + nm, align_bytes=64)
            scales = quant.tile([P, CW], U8, tag="scales" + nm, name="scales" + nm, align_bytes=64)
            nc.vector.quantize_mx(out=codes[:].bitcast(FP8X4), scales=scales[:], in_=kept[("grouped" + nm, c)][:])
            kept[("mx" + nm, c)] = (codes, scales)

        def matmul_mx(out, lhs, rhs, first, last):
            nc.tensor.matmul_mx(
                out=out,
                lhsT=lhs[0].bitcast(FP8X4),
                lhsT_scale=lhs[1],
                rhs=rhs[0].bitcast(FP8X4),
                rhs_scale=rhs[1],
                start=first,
                stop=last,
            )

        def weight(g):
            return w_codes[:, g * H : (g + 1) * H], w_scales[:, g * H : (g + 1) * H]

        def project_d(c):
            if absent(c):
                return
            codes, scales = kept[("mxc", c)]
            bank = bank_tile("d")
            for t in range(TPC):
                x_tile = codes[:, part(t)], scales[:, part(t)]
                matmul_mx(bank[:, part(t)], x_tile, weight(W_F), True, False)
                matmul_mx(bank[:, part(t)], x_tile, weight(W_NI), False, True)
            kept[("d_sum", c)] = bank

        def project(c, name):
            if absent(c):
                return
            g, nm = {"i": (W_I, "c"), "k": (W_K, "c"), "q": (W_Q, "c"), "v": (W_V, "l"), "o": (W_O, "l")}[name]
            codes, scales = kept[("mx" + nm, c)]
            bank = bank_tile(name)
            matmul_mx(bank[:], weight(g), (codes[:], scales[:]), True, True)
            kept[(name + "_sum", c)] = bank

        def leave(c, name):
            if absent(c):
                return
            func, bias, scale = {
                "i": (ACT.Identity, bias_col[:, B_I : B_I + 1], 1.0),
                "k": (ACT.Identity, bk_scaled[:], k_scale),
                "q": (ACT.Identity, bias_col[:, B_Q : B_Q + 1], 1.0),
                "v": (ACT.Identity, bias_col[:, B_V : B_V + 1], 1.0),
                "o": (ACT.Tanh, bo_half[:], 0.5),
            }[name]
            nc.scalar.activation(
                out=new(work, name + "_cols", c)[:], in_=kept[(name + "_sum", c)][:], func=func, bias=bias, scale=scale
            )

        def to_rows(c, name):
            if absent(c):
                return
            cols = kept[(name + "_cols", c)]
            bank = bank_tile("xl0" if name == "q" and c == CHUNKS - 1 else name + "_rows")
            for t in range(TPC):
                nc.tensor.transpose(bank[:, part(t)], cols[:, part(t)], ident[:])
            kept[(name, c)] = bank

        m_shifted = const.tile([P, TILES * H], F32)

        def shift_m(c):
            if absent(c):
                return
            columns = slice(c * CW, (c + 1) * CW)
            nc.vector.tensor_tensor(
                out=by_tile(m_shifted[:, columns]),
                in0=by_tile(m_all[:, columns]),
                in1=bf_minus_bi[:].unsqueeze(1).to_broadcast([P, TPC, H]),
                op=ALU.add,
            )
            kept[("m_shifted", c)] = m_shifted[:, columns]

        def two(engine, pool, out_name, c, a, b, op):
            if absent(c):
                return
            engine.tensor_tensor(out=new(pool, out_name, c)[:], in0=kept[(a, c)][:], in1=kept[(b, c)][:], op=op)

        def three(pool, out_name, c, a, scalar, op0, b, op1):
            if absent(c):
                return
            nc.vector.scalar_tensor_tensor(
                out=new(pool, out_name, c)[:], in0=kept[(a, c)][:], scalar=scalar, in1=kept[(b, c)][:], op0=op0, op1=op1
            )

        def d_new(c):
            two(nc.vector, work, "d", c, "d_sum", "m_shifted", ALU.add)

        def exponential(c, out_name, sign):
            if absent(c):
                return
            nc.scalar.activation(out=new(work, out_name, c)[:], in_=kept[("d", c)][:], func=ACT.Exp, scale=sign)

        def m_new(c):
            three(outs, "m_t", c, "d", 0.0, ALU.max, "i", ALU.add)
            if not absent(c):
                store(c, "m")

        def ik(c):
            three(work, "ik", c, "exp_minus_d", 1.0, ALU.min, "k", ALU.mult)

        def forget(c, state):
            three(work, "f" + state, c, "exp_d", 1.0, ALU.min, state + "_prev", ALU.mult)

        def ikv(c):
            two(nc.vector, work, "ikv", c, "v", "ik", ALU.mult)

        def state_new(c, state, update):
            two(nc.gpsimd, outs, state + "_t", c, "f" + state, update, ALU.add)
            if not absent(c):
                store(c, state)

        def times_q(c, state):
            two(nc.vector, work, state + "q", c, "q", state + "_t", ALU.mult)

        def open_gate(c):
            three(work, "ocq", c, "o", 1.0, ALU.add, "cq", ALU.mult)

        def sum_of_squares(c):
            if absent(c):
                return
            squares = const.tile([P, CW], F32, tag="squares", name="squares")
            total = new_column("total", c)
            for t in range(TPC):
                nc.scalar.activation(
                    out=squares[:, part(t)],
                    in_=kept[("nq", c)][:, part(t)],
                    func=ACT.Square,
                    scale=2.0,
                    accum_out=total[:, t : t + 1],
                )

        def square_root(c):
            if absent(c):
                return
            nc.gpsimd.tensor_tensor(out=new_column("norm", c)[:], in0=kept[("total", c)][:], in1=half[:], op=ALU.pow)

        def add_epsilon(c):
            if absent(c):
                return
            nc.vector.tensor_scalar_add(out=new_column("denom", c)[:], in0=kept[("norm", c)][:], scalar1=2.0e-6)

        def reciprocal(c):
            if absent(c):
                return
            nc.vector.reciprocal(out=new_column("scale", c)[:], in_=kept[("denom", c)][:])

        def scale_rows(c):
            if absent(c):
                return
            h_t = new(outs, "h_t", c)
            for t in range(TPC):
                nc.vector.tensor_scalar_mul(
                    out=h_t[:, part(t)], in0=kept[("ocq", c)][:, part(t)], scalar1=kept[("scale", c)][:, t : t + 1]
                )
            store(c, "h")

        def keep_clock(count):
            bank = bank_tile("v_rows")
            for n in range(count):
                nc.tensor.matmul(out=bank[:, 0:P], lhsT=ident_bf[:], rhs=ident_bf[:], start=True, stop=True)

        keep_clock(18)
        transpose_x(0, "c", 0)
        transpose_x(0, "c", 1)
        spread = bank_tile("q_rows")
        nc.tensor.transpose(spread[:, 0:P], bias_f32[:], ident[:])
        for n, b in enumerate((B_I, B_F)):
            nc.tensor.matmul(
                out=spread[:, (n + 1) * P : (n + 2) * P],
                lhsT=ident_bf[:, b : b + 1].to_broadcast([P, P]),
                rhs=bias_rows[:],
                start=True,
                stop=True,
            )
        bias_col = const.tile([P, 6], F32)
        nc.vector.tensor_copy(out=bias_col[:], in_=spread[:, 0:6])
        bi_row = const.tile([P, H], F32)
        nc.vector.tensor_copy(out=bi_row[:], in_=spread[:, P : 2 * P])
        bo_half = const.tile([P, 1], F32)
        nc.vector.tensor_scalar_mul(out=bo_half[:], in0=bias_col[:, B_O : B_O + 1], scalar1=0.5)
        bk_scaled = const.tile([P, 1], F32)
        nc.vector.tensor_scalar_mul(out=bk_scaled[:], in0=bias_col[:, B_K : B_K + 1], scalar1=k_scale)
        bf_minus_bi = const.tile([P, H], F32)
        nc.vector.tensor_tensor(out=bf_minus_bi[:], in0=spread[:, 2 * P : 3 * P], in1=bi_row[:], op=ALU.subtract)
        group_weights(nc.vector.tensor_copy, W_F, 0)
        nc.vector.tensor_scalar_mul(out=w_grouped[:, W_NI], in0=w_raw[:, 1].rearrange("p j c -> p c j"), scalar1=-1.0)
        quantise_weights(W_F, W_NI + 1)

        for j in range(-2, CHUNKS + 1):
            ahead, gates, cell, last, done = j + 2, j + 1, j, j - 1, j - 2
            head = j == -2
            tail = j == CHUNKS - 1

            leave(gates, "k")
            leave(gates, "i")
            ik(cell)
            to_rows(cell, "v")
            forget(cell, "n")
            forget(cell, "c")
            state_new(cell, "n", "ik")

            for nm in ("c", "l"):
                for half_no in range(2):
                    if not (head and nm == "c"):
                        transpose_x(ahead, nm, half_no)
                    regroup_x(ahead, nm, half_no)
                if head and nm == "c":
                    group_weights(nc.scalar.copy, W_I, 1)
            load_x(j + 6, "c")
            load_x(j + 6, "l")

            to_rows(last, "o")
            ikv(cell)
            if last < CHUNKS - 1:
                times_q(last, "n")
            state_new(cell, "c", "ikv")
            add_epsilon(done)

            project(gates, "v")
            leave(gates, "v")
            if last < CHUNKS - 1:
                sum_of_squares(last)
            project(gates, "o")
            leave(gates, "o")
            project(gates, "q")
            leave(gates, "q")

            times_q(last, "c")
            d_new(gates)
            exponential(gates, "exp_minus_d", -1.0)
            exponential(gates, "exp_d", 1.0)
            to_rows(gates, "i")
            open_gate(last)
            quantise_x(ahead, "c")
            if head:
                group_weights(nc.vector.tensor_copy, W_K, 2)
                quantise_weights(W_I, W_K + 1)
                shift_m(0)
            to_rows(cell, "q")
            to_rows(gates, "k")
            if tail:
                times_q(cell, "n")
                sum_of_squares(cell)
            reciprocal(done)

            if head:
                keep_clock(8)
            project_d(ahead)
            project(ahead, "k")
            quantise_x(ahead, "l")
            if head:
                group_weights(nc.scalar.copy, W_Q, 3)
                group_weights(nc.scalar.copy, W_V, 4)
                group_weights(nc.vector.tensor_copy, W_O, 5)
                quantise_weights(W_Q, W_Q + 1)
                quantise_weights(W_V, W_O + 1)
            if last < CHUNKS - 1:
                square_root(last)
            if tail:
                square_root(cell)
            project(ahead, "i")
            m_new(gates)
            scale_rows(done)
            if last == CHUNKS - 1:
                add_epsilon(last)
                reciprocal(last)
                scale_rows(last)
            shift_m(j + 3)
